import numpy as np
import ml_dtypes


def mxq(x, axis, fmt="e4m3"):
    dtype, down = {"e4m3": (ml_dtypes.float8_e4m3fn, 7), "e5m2": (ml_dtypes.float8_e5m2, 14)}[fmt]
    v = np.moveaxis(np.asarray(x, np.float32).astype(ml_dtypes.bfloat16).astype(np.float64), axis, -1)
    blocks = v.reshape(v.shape[:-1] + (-1, 32))
    amax = np.abs(blocks).max(-1, keepdims=True)
    byte = np.maximum(np.where(amax > 0, np.frexp(amax)[1] - 1 + 127, 0) - down, 1)
    scale = np.exp2(byte - 127.0)
    codes = (blocks / scale).astype(np.float32).astype(dtype).astype(np.float64)
    return np.moveaxis((codes * scale).reshape(v.shape), -1, axis)


WIDE = False


def mx_kscale(k):
    if not WIDE:
        return np.ones(k)
    levels = np.array([10, -10, 5, -5, 0])
    if k % 512:
        return np.exp2(np.random.permutation(np.resize(levels, k // 32))).repeat(32)
    a = np.empty((k // 512, 16))
    for p in range(k // 512):
        a[p, :8] = np.random.permutation(np.resize(levels, 8))
        for g in range(8):
            far = levels[np.abs(levels - a[p, g]) >= 10]
            a[p, g + 8] = far[np.random.randint(len(far))]
    return np.exp2(a.ravel()).repeat(32)


BF16 = ml_dtypes.bfloat16


def bf(x):
    return np.asarray(x, np.float32).astype(BF16)


def f64(x):
    return np.asarray(x).astype(np.float64)


B, S, D, H, HD = 4, 128, 1536, 16, 96
DPA = HD // 6


def build_rope_freqs():
    return 1.0 / (10000.0 ** (np.arange(DPA) / DPA))


def apply_rope_3d(t, coords, freqs):
    theta = (coords[..., None] * freqs).reshape(*coords.shape[:-1], -1)[:, None]
    cos, sin = np.cos(theta), np.sin(theta)
    tp = t.reshape(*t.shape[:-1], t.shape[-1] // 2, 2)
    t1, t2 = tp[..., 0], tp[..., 1]
    out = np.stack([t1 * cos - t2 * sin, t1 * sin + t2 * cos], axis=-1)
    return out.reshape(t.shape)


def setup_inputs():
    s = mx_kscale(D)
    return {'x': bf(np.random.standard_normal((B, S, D)) * s),
            'coords': bf(np.random.standard_normal((B, S, 3))),
            'W_qkv': bf(np.random.standard_normal((3 * H * HD, D)) / np.sqrt(D) / s)}


def reference(x, coords, W_qkv):
    freqs = build_rope_freqs()
    c = f64(coords)
    qkv = mxq(f64(x), 2, 'e4m3') @ mxq(f64(W_qkv), 1, 'e4m3').T
    qkv = qkv.reshape(B, S, 3, H, HD)
    q, k, v = (qkv[:, :, i].transpose(0, 2, 1, 3) for i in range(3))
    return apply_rope_3d(q, c, freqs), apply_rope_3d(k, c, freqs), v

@@ -1,0 +1,245 @@
+import math
+from contextlib import ExitStack
+
+import concourse.mybir as mybir
+from concourse.masks import make_identity
+
+F32 = mybir.dt.float32
+BF16 = mybir.dt.bfloat16
+U32 = mybir.dt.uint32
+U8 = mybir.dt.uint8
+FP8X4 = mybir.dt.float8_e4m3fn_x4
+ALU = mybir.AluOpType
+ACT = mybir.ActivationFunctionType
+
+P = 128
+BATCH = 4
+FEATURES = 1536
+HEADS = 16
+HEAD_DIM = 96
+PAIRS = HEAD_DIM // 2
+FREQS = HEAD_DIM // 6
+K_PASS = 512
+PASSES = FEATURES // K_PASS
+PASS_WORDS = K_PASS // 2
+
+GROUP_HEADS = 4
+GROUP_COLS = GROUP_HEADS * HEAD_DIM
+GROUP_TILES = GROUP_COLS // P
+GROUPS_PER_OUTPUT = HEADS // GROUP_HEADS
+PARTS = ((0, 2 * P), (2 * P, GROUP_COLS))
+LEAD = 3
+
+FLOPS = 2 * BATCH * P * FEATURES * 3 * HEADS * HEAD_DIM
+
+TURN_HI = 6.28125
+TURN_MID = 4059.0 / 2097152.0
+TURN_LO = 2.0 * math.pi - TURN_HI - TURN_MID
+ROUND_MAGIC = 12582912.0
+PI_BELOW = 3.1415925
+
+
+def rotation_arguments(nc, const, coords_sb):
+    theta = const.tile([P, BATCH, PAIRS], F32)
+    theta_by_freq = theta[:].rearrange("s b (a j) -> s (b a) j", j=FREQS)
+    for j in range(FREQS):
+        nc.vector.tensor_scalar(
+            out=theta_by_freq[:, :, j],
+            in0=coords_sb[:].rearrange("s b a -> s (b a)"),
+            scalar1=10000.0 ** (-j / FREQS),
+            scalar2=None,
+            op0=ALU.mult,
+        )
+
+    turns = const.tile([P, BATCH, PAIRS], F32)
+    nc.vector.tensor_scalar(
+        out=turns[:], in0=theta[:], scalar1=0.5 / math.pi, scalar2=ROUND_MAGIC, op0=ALU.mult, op1=ALU.add
+    )
+    nc.vector.tensor_scalar(out=turns[:], in0=turns[:], scalar1=ROUND_MAGIC, scalar2=None, op0=ALU.subtract)
+    reduced = const.tile([P, BATCH, PAIRS], F32)
+    nc.vector.scalar_tensor_tensor(
+        out=reduced[:], in0=turns[:], scalar=-TURN_HI, in1=theta[:], op0=ALU.mult, op1=ALU.add
+    )
+    for piece in (TURN_MID, TURN_LO):
+        nc.vector.scalar_tensor_tensor(
+            out=reduced[:], in0=turns[:], scalar=-piece, in1=reduced[:], op0=ALU.mult, op1=ALU.add
+        )
+    nc.vector.tensor_scalar(
+        out=reduced[:], in0=reduced[:], scalar1=-PI_BELOW, scalar2=PI_BELOW, op0=ALU.max, op1=ALU.min
+    )
+    magnitude = const.tile([P, BATCH, PAIRS], F32)
+    nc.vector.scalar_tensor_tensor(
+        out=magnitude[:], in0=reduced[:], scalar=-1.0, in1=reduced[:], op0=ALU.mult, op1=ALU.max
+    )
+
+    angle = const.tile([P, BATCH, PAIRS, 2, 2], F32)
+    for i in range(2):
+        nc.vector.tensor_scalar(
+            out=angle[:, :, :, i, i], in0=magnitude[:], scalar1=-1.0, scalar2=0.5 * math.pi,
+            op0=ALU.mult, op1=ALU.add,
+        )
+    nc.vector.tensor_copy(out=angle[:, :, :, 0, 1], in_=reduced[:])
+    nc.vector.tensor_scalar(out=angle[:, :, :, 1, 0], in0=reduced[:], scalar1=-1.0, scalar2=None, op0=ALU.mult)
+    return angle
+
+
+def flip_rows(nc, flip_psum, stage, identity, row_tiles, g):
+    cols = P * len(row_tiles)
+    flipped = flip_psum.tile([P, 2, cols], F32, tag="flipped")
+    for u in range(2):
+        first = PASS_WORDS * g + u
+        for t, rows in enumerate(row_tiles):
+            nc.tensor.transpose(
+                flipped[:, u, P * t : P * t + P], rows[:, first : PASS_WORDS * (g + 1) : 2], identity[:]
+            )
+    grouped = stage.tile([P, 4 * cols], BF16, tag="grouped", align_bytes=64)
+    nc.scalar.copy(
+        out=grouped[:].bitcast(F32).rearrange("q (c u) -> q c u", u=2),
+        in_=flipped[:].rearrange("q u c -> q c u"),
+    )
+    return grouped
+
+
+def tile_ropeattention_pa_kernel(tc, x, coords, W_qkv, out_0, out_1, out_2):
+    nc = tc.nc
+    outputs = (out_0, out_1, out_2)
+    groups = [(which, quarter) for quarter in range(GROUPS_PER_OUTPUT) for which in (0, 2, 1)]
+    units = []
+    for quarter in range(GROUPS_PER_OUTPUT):
+        rotated = [((which, quarter), b) for which in (0, 1) for b in range(BATCH)]
+        for b in range(BATCH):
+            units.extend([rotated[2 * b], rotated[2 * b + 1], ((2, quarter), b)])
+    pieces = [(g, lo, hi) for g in range(PASSES) for lo, hi in PARTS]
+    halves = (pieces[:3], pieces[3:])
+    half_groups = [(group, half) for group in groups for half in range(2)]
+
+    with ExitStack() as ctx:
+        const = ctx.enter_context(tc.tile_pool(name="const", bufs=1))
+        weights = ctx.enter_context(tc.tile_pool(name="weights", bufs=9))
+        stage = ctx.enter_context(tc.tile_pool(name="stage", bufs=6))
+        packed = ctx.enter_context(tc.tile_pool(name="packed", bufs=4))
+        work = ctx.enter_context(tc.tile_pool(name="work", bufs=6))
+        results = ctx.enter_context(tc.tile_pool(name="results", bufs=40))
+        flip_psum = ctx.enter_context(tc.psum_pool(name="flip_psum", bufs=4))
+        acc_psum = ctx.enter_context(tc.psum_pool(name="acc_psum", bufs=4))
+        ctx.enter_context(tc.manual_schedule())
+
+        coords_sb = const.tile([P, BATCH, 3], BF16)
+        nc.scalar.dma_start(out=coords_sb[:], in_=coords.rearrange("b s a -> s b a"))
+        x_raw = const.tile([P, BATCH, FEATURES], BF16)
+        for b in range(BATCH):
+            nc.sync.dma_start(out=x_raw[:, b, :], in_=x[b])
+        w_raw = {}
+        for which, quarter in groups:
+            first_row = which * HEADS * HEAD_DIM + quarter * GROUP_COLS
+            w_rows = weights.tile([P, GROUP_TILES, FEATURES], BF16, tag="w_rows")
+            nc.sync.dma_start(
+                out=w_rows[:],
+                in_=W_qkv[first_row : first_row + GROUP_COLS, :].rearrange("(t p) k -> p t k", p=P),
+            )
+            w_raw[(which, quarter)] = w_rows
+
+        warm = const.tile([P, 1], F32)
+        nc.vector.memset(warm[:], 0.0)
+        nc.scalar.activation(out=warm[:], in_=warm[:], func=ACT.Sin)
+
+        identity = const.tile([P, P], F32)
+        make_identity(nc, identity[:])
+        angle = rotation_arguments(nc, const, coords_sb)
+
+        x_codes = const.tile([P, PASSES, BATCH * P], U32, align_bytes=64)
+        x_scales = const.tile([P, PASSES, BATCH * P], U8, align_bytes=64)
+        x_words = x_raw[:].bitcast(F32)
+        for b in range(0, BATCH, 2):
+            flipped_x = [
+                flip_rows(nc, flip_psum, stage, identity, [x_words[:, b, :], x_words[:, b + 1, :]], g)
+                for g in range(PASSES)
+            ]
+            for g in range(PASSES):
+                nc.vector.quantize_mx(
+                    out=x_codes[:, g, P * b : P * b + 2 * P].bitcast(FP8X4),
+                    scales=x_scales[:, g, P * b : P * b + 2 * P],
+                    in_=flipped_x[g][:],
+                )
+
+        def flip_half(group, half):
+            w_words = w_raw[group][:].bitcast(F32)
+            return [
+                flip_rows(nc, flip_psum, stage, identity, [w_words[:, t, :] for t in range(lo // P, hi // P)], g)
+                for g, lo, hi in halves[half]
+            ]
+
+        def quantise_half(half, flipped_w, w_codes, w_scales):
+            for (g, lo, hi), grouped in zip(halves[half], flipped_w):
+                nc.vector.quantize_mx(
+                    out=w_codes[:, g, lo:hi].bitcast(FP8X4), scales=w_scales[:, g, lo:hi], in_=grouped[:]
+                )
+
+        def multiply(b, w_codes, w_scales):
+            acc = acc_psum.tile([P, GROUP_COLS], F32, tag="acc")
+            for lo, hi in PARTS:
+                for g in range(PASSES):
+                    nc.tensor.matmul_mx(
+                        out=acc[:, lo:hi],
+                        lhsT=x_codes[:, g, P * b : P * b + P].bitcast(FP8X4),
+                        lhsT_scale=x_scales[:, g, P * b : P * b + P],
+                        rhs=w_codes[:, g, lo:hi].bitcast(FP8X4),
+                        rhs_scale=w_scales[:, g, lo:hi],
+                        start=(g == 0),
+                        stop=(g == PASSES - 1),
+                    )
+            return acc
+
+        def multiply_by_table(b, acc):
+            products = work.tile([P, 2, GROUP_HEADS, PAIRS, 2], F32, tag="products")
+            shape = [P, GROUP_HEADS, PAIRS, 2, 2]
+            nc.vector.tensor_tensor(
+                out=products[:].rearrange("s w h n e -> s h n w e"),
+                in0=acc[:].rearrange("s (h n w) -> s h n w", h=GROUP_HEADS, w=2).unsqueeze(4).to_broadcast(shape),
+                in1=rot[:, b].unsqueeze(1).to_broadcast(shape),
+                op=ALU.mult,
+            )
+            return products
+
+        def store(group, b, result):
+            which, quarter = group
+            first_head = quarter * GROUP_HEADS
+            nc.sync.dma_start(
+                out=outputs[which][b, first_head : first_head + GROUP_HEADS].rearrange("h s d -> s h d"),
+                in_=result[:].rearrange("s (h d) -> s h d", h=GROUP_HEADS),
+            )
+
+        operands = {}
+
+        def prepare(group, half):
+            if half == 0:
+                w_codes = packed.tile([P, PASSES, GROUP_COLS], U32, tag="w_codes", align_bytes=64)
+                w_scales = packed.tile([P, PASSES, GROUP_COLS], U8, tag="w_scales", align_bytes=64)
+                operands[group] = (w_codes, w_scales)
+            quantise_half(half, flip_half(group, half), *operands[group])
+
+        for group, half in half_groups[:LEAD]:
+            prepare(group, half)
+        rot = const.tile([P, BATCH, PAIRS, 2, 2], F32)
+        nc.scalar.activation(out=rot[:], in_=angle[:], func=ACT.Sin)
+
+        for step in range(len(units) // 2):
+            for group, half in half_groups[step + LEAD : step + LEAD + 1]:
+                prepare(group, half)
+            pair = units[2 * step : 2 * step + 2]
+            accs = [multiply(b, *operands[group]) for group, b in pair]
+            products = [
+                multiply_by_table(b, acc) if group[0] != 2 else None for (group, b), acc in zip(pair, accs)
+            ]
+            for (group, b), acc, planes in zip(pair, accs, products):
+                result = results.tile([P, GROUP_COLS], F32, tag="result")
+                if planes is None:
+                    nc.scalar.copy(out=result[:], in_=acc[:])
+                else:
+                    nc.gpsimd.tensor_tensor(
+                        out=result[:],
+                        in0=planes[:, 0].rearrange("s h n e -> s (h n e)"),
+                        in1=planes[:, 1].rearrange("s h n e -> s (h n e)"),
+                        op=ALU.add,
+                    )
+                store(group, b, result)

@@ -22,15 +22,18 @@ FREQS = HEAD_DIM // 6
 K_PASS = 512
 PASSES = FEATURES // K_PASS
 PASS_WORDS = K_PASS // 2
+OUT_COLS = HEADS * HEAD_DIM
 
-GROUP_HEADS = 4
-GROUP_COLS = GROUP_HEADS * HEAD_DIM
-GROUP_TILES = GROUP_COLS // P
-GROUPS_PER_OUTPUT = HEADS // GROUP_HEADS
-PARTS = ((0, 2 * P), (2 * P, GROUP_COLS))
-LEAD = 3
+GROUP_COLS = 512
+TILES = GROUP_COLS // P
+GROUPS_PER_OUTPUT = OUT_COLS // GROUP_COLS
+WHOLE_HEADS = GROUP_COLS // HEAD_DIM
+WHOLE = WHOLE_HEADS * HEAD_DIM
+REST_PAIRS = (GROUP_COLS - WHOLE) // 2
+FIRST_SPREAD = 3
+SPREAD_TILES = 3
 
-FLOPS = 2 * BATCH * P * FEATURES * 3 * HEADS * HEAD_DIM
+FLOPS = 2 * BATCH * P * FEATURES * 3 * OUT_COLS
 
 TURN_HI = 6.28125
 TURN_MID = 4059.0 / 2097152.0
@@ -83,61 +86,56 @@ def rotation_arguments(nc, const, coords_sb):
     return angle
 
 
-def flip_rows(nc, flip_psum, stage, identity, row_tiles, g):
-    cols = P * len(row_tiles)
-    flipped = flip_psum.tile([P, 2, cols], F32, tag="flipped")
-    for u in range(2):
-        first = PASS_WORDS * g + u
-        for t, rows in enumerate(row_tiles):
-            nc.tensor.transpose(
-                flipped[:, u, P * t : P * t + P], rows[:, first : PASS_WORDS * (g + 1) : 2], identity[:]
-            )
-    grouped = stage.tile([P, 4 * cols], BF16, tag="grouped", align_bytes=64)
-    nc.scalar.copy(
-        out=grouped[:].bitcast(F32).rearrange("q (c u) -> q c u", u=2),
-        in_=flipped[:].rearrange("q u c -> q c u"),
-    )
-    return grouped
-
-
 def tile_ropeattention_pa_kernel(tc, x, coords, W_qkv, out_0, out_1, out_2):
     nc = tc.nc
     outputs = (out_0, out_1, out_2)
-    groups = [(which, quarter) for quarter in range(GROUPS_PER_OUTPUT) for which in (0, 2, 1)]
-    units = []
-    for quarter in range(GROUPS_PER_OUTPUT):
-        rotated = [((which, quarter), b) for which in (0, 1) for b in range(BATCH)]
-        for b in range(BATCH):
-            units.extend([rotated[2 * b], rotated[2 * b + 1], ((2, quarter), b)])
-    pieces = [(g, lo, hi) for g in range(PASSES) for lo, hi in PARTS]
-    halves = (pieces[:3], pieces[3:])
-    half_groups = [(group, half) for group in groups for half in range(2)]
+    groups = [(which, c) for c in range(GROUPS_PER_OUTPUT) for which in range(3)]
+    last = len(groups) - 1
 
     with ExitStack() as ctx:
         const = ctx.enter_context(tc.tile_pool(name="const", bufs=1))
-        weights = ctx.enter_context(tc.tile_pool(name="weights", bufs=9))
-        stage = ctx.enter_context(tc.tile_pool(name="stage", bufs=6))
-        packed = ctx.enter_context(tc.tile_pool(name="packed", bufs=4))
-        work = ctx.enter_context(tc.tile_pool(name="work", bufs=6))
-        results = ctx.enter_context(tc.tile_pool(name="results", bufs=40))
+        rows_pool = ctx.enter_context(tc.tile_pool(name="rows_pool", bufs=11))
+        spread_pool = ctx.enter_context(tc.tile_pool(name="spread_pool", bufs=5))
+        stage_x = ctx.enter_context(tc.tile_pool(name="stage_x", bufs=2))
+        stage = ctx.enter_context(tc.tile_pool(name="stage", bufs=5))
+        packed = ctx.enter_context(tc.tile_pool(name="packed", bufs=2))
+        work = ctx.enter_context(tc.tile_pool(name="work", bufs=3))
+        results = ctx.enter_context(tc.tile_pool(name="results", bufs=1))
         flip_psum = ctx.enter_context(tc.psum_pool(name="flip_psum", bufs=4))
         acc_psum = ctx.enter_context(tc.psum_pool(name="acc_psum", bufs=4))
         ctx.enter_context(tc.manual_schedule())
 
         coords_sb = const.tile([P, BATCH, 3], BF16)
         nc.scalar.dma_start(out=coords_sb[:], in_=coords.rearrange("b s a -> s b a"))
-        x_raw = const.tile([P, BATCH, FEATURES], BF16)
-        for b in range(BATCH):
-            nc.sync.dma_start(out=x_raw[:, b, :], in_=x[b])
-        w_raw = {}
-        for which, quarter in groups:
-            first_row = which * HEADS * HEAD_DIM + quarter * GROUP_COLS
-            w_rows = weights.tile([P, GROUP_TILES, FEATURES], BF16, tag="w_rows")
-            nc.sync.dma_start(
-                out=w_rows[:],
-                in_=W_qkv[first_row : first_row + GROUP_COLS, :].rearrange("(t p) k -> p t k", p=P),
-            )
-            w_raw[(which, quarter)] = w_rows
+
+        x_rows = []
+        for i in range(BATCH // 2):
+            x_pair = rows_pool.tile([P, 2, FEATURES], BF16, tag="rows")
+            x_rows.append(x_pair)
+
+        def load_x(b):
+            nc.sync.dma_start(out=x_rows[b // 2][:, b % 2, :], in_=x[b])
+
+        w_rows = {}
+
+        def load_group(i, tiles_at_once):
+            which, c = groups[i]
+            for half in range(2):
+                pair = rows_pool.tile([P, 2, FEATURES], BF16, tag="rows")
+                w_rows[(i, half)] = pair
+                for t in range(0, 2, tiles_at_once):
+                    row = which * OUT_COLS + c * GROUP_COLS + (2 * half + t) * P
+                    nc.sync.dma_start(
+                        out=pair[:, t : t + tiles_at_once, :],
+                        in_=W_qkv[row : row + tiles_at_once * P, :].rearrange("(t p) k -> p t k", p=P),
+                    )
+
+        load_x(0)
+        load_group(0, 1)
+        for b in range(1, BATCH):
+            load_x(b)
+        for i in range(1, last + 1):
+            load_group(i, 2)
 
         warm = const.tile([P, 1], F32)
         nc.vector.memset(warm[:], 0.0)
@@ -149,97 +147,151 @@ def tile_ropeattention_pa_kernel(tc, x, coords, W_qkv, out_0, out_1, out_2):
 
         x_codes = const.tile([P, PASSES, BATCH * P], U32, align_bytes=64)
         x_scales = const.tile([P, PASSES, BATCH * P], U8, align_bytes=64)
-        x_words = x_raw[:].bitcast(F32)
-        for b in range(0, BATCH, 2):
-            flipped_x = [
-                flip_rows(nc, flip_psum, stage, identity, [x_words[:, b, :], x_words[:, b + 1, :]], g)
-                for g in range(PASSES)
-            ]
+
+        def every_second(words, g, u):
+            return words[:, PASS_WORDS * g + u : PASS_WORDS * (g + 1) : 2]
+
+        def flip_x(b):
+            words = x_rows[b // 2][:].bitcast(F32)[:, b % 2, :]
+            grouped = stage_x.tile([P, PASSES, 4 * P], BF16, tag="grouped_x", align_bytes=64)
+            for g0, g1 in ((0, 2), (2, 3)):
+                flipped = flip_psum.tile([P, g1 - g0, 2, P], F32, tag="flipped")
+                for g in range(g0, g1):
+                    for u in range(2):
+                        nc.tensor.transpose(flipped[:, g - g0, u, :], every_second(words, g, u), identity[:])
+                nc.scalar.copy(
+                    out=grouped[:, g0:g1, :].bitcast(F32).rearrange("q g (c u) -> q g c u", u=2),
+                    in_=flipped[:].rearrange("q g u c -> q g c u"),
+                )
+            return grouped
+
+        def quantise_x(b, grouped):
             for g in range(PASSES):
                 nc.vector.quantize_mx(
-                    out=x_codes[:, g, P * b : P * b + 2 * P].bitcast(FP8X4),
-                    scales=x_scales[:, g, P * b : P * b + 2 * P],
-                    in_=flipped_x[g][:],
+                    out=x_codes[:, g, P * b : P * b + P].bitcast(FP8X4),
+                    scales=x_scales[:, g, P * b : P * b + P],
+                    in_=grouped[:, g, :],
                 )
 
-        def flip_half(group, half):
-            w_words = w_raw[group][:].bitcast(F32)
-            return [
-                flip_rows(nc, flip_psum, stage, identity, [w_words[:, t, :] for t in range(lo // P, hi // P)], g)
-                for g, lo, hi in halves[half]
-            ]
+        spread = {}
 
-        def quantise_half(half, flipped_w, w_codes, w_scales):
-            for (g, lo, hi), grouped in zip(halves[half], flipped_w):
-                nc.vector.quantize_mx(
-                    out=w_codes[:, g, lo:hi].bitcast(FP8X4), scales=w_scales[:, g, lo:hi], in_=grouped[:]
-                )
+        def spread_tile(i, t):
+            tile = spread_pool.tile([P, PASSES, 2, P], F32, tag="spread")
+            words = w_rows[(i, t // 2)][:].bitcast(F32)[:, t % 2, :]
+            nc.scalar.copy(out=tile[:], in_=words.rearrange("r (g q u) -> r g u q", g=PASSES, u=2))
+            spread[(i, t)] = tile
 
-        def multiply(b, w_codes, w_scales):
-            acc = acc_psum.tile([P, GROUP_COLS], F32, tag="acc")
-            for lo, hi in PARTS:
-                for g in range(PASSES):
-                    nc.tensor.matmul_mx(
-                        out=acc[:, lo:hi],
-                        lhsT=x_codes[:, g, P * b : P * b + P].bitcast(FP8X4),
-                        lhsT_scale=x_scales[:, g, P * b : P * b + P],
-                        rhs=w_codes[:, g, lo:hi].bitcast(FP8X4),
-                        rhs_scale=w_scales[:, g, lo:hi],
-                        start=(g == 0),
-                        stop=(g == PASSES - 1),
-                    )
-            return acc
+        def flip_bank(i, g, half):
+            flipped = flip_psum.tile([P, 2, 2 * P], F32, tag="flipped")
+            for u in range(2):
+                for t in range(2):
+                    if (i, 2 * half + t) in spread:
+                        words = spread[(i, 2 * half + t)][:, g, u, :]
+                    else:
+                        words = every_second(w_rows[(i, half)][:].bitcast(F32)[:, t, :], g, u)
+                    nc.tensor.transpose(flipped[:, u, P * t : P * t + P], words, identity[:])
+            return flipped
 
-        def multiply_by_table(b, acc):
-            products = work.tile([P, 2, GROUP_HEADS, PAIRS, 2], F32, tag="products")
-            shape = [P, GROUP_HEADS, PAIRS, 2, 2]
-            nc.vector.tensor_tensor(
-                out=products[:].rearrange("s w h n e -> s h n w e"),
-                in0=acc[:].rearrange("s (h n w) -> s h n w", h=GROUP_HEADS, w=2).unsqueeze(4).to_broadcast(shape),
-                in1=rot[:, b].unsqueeze(1).to_broadcast(shape),
-                op=ALU.mult,
-            )
-            return products
-
-        def store(group, b, result):
-            which, quarter = group
-            first_head = quarter * GROUP_HEADS
-            nc.sync.dma_start(
-                out=outputs[which][b, first_head : first_head + GROUP_HEADS].rearrange("h s d -> s h d"),
-                in_=result[:].rearrange("s (h d) -> s h d", h=GROUP_HEADS),
+        def empty_bank(copy, flipped, grouped, half):
+            copy(
+                out=grouped[:].bitcast(F32)[:, 512 * half : 512 * half + 512].rearrange("q (c u) -> q c u", u=2),
+                in_=flipped[:].rearrange("q u c -> q c u"),
             )
 
         operands = {}
 
-        def prepare(group, half):
-            if half == 0:
-                w_codes = packed.tile([P, PASSES, GROUP_COLS], U32, tag="w_codes", align_bytes=64)
-                w_scales = packed.tile([P, PASSES, GROUP_COLS], U8, tag="w_scales", align_bytes=64)
-                operands[group] = (w_codes, w_scales)
-            quantise_half(half, flip_half(group, half), *operands[group])
+        def prepare(i, order, on_vector):
+            w_codes = packed.tile([P, PASSES, GROUP_COLS], U32, tag="w_codes", align_bytes=64)
+            w_scales = packed.tile([P, PASSES, GROUP_COLS], U8, tag="w_scales", align_bytes=64)
+            operands[i] = (w_codes, w_scales)
+            grouped = []
+            for g in range(PASSES):
+                grouped_g = stage.tile([P, 4 * GROUP_COLS], BF16, tag="grouped", align_bytes=64)
+                grouped.append(grouped_g)
+            for n, (g, half) in enumerate(order):
+                copy = nc.vector.tensor_copy if n >= len(order) - on_vector else nc.scalar.copy
+                empty_bank(copy, flip_bank(i, g, half), grouped[g], half)
+            for g in range(PASSES):
+                nc.vector.quantize_mx(
+                    out=w_codes[:, g, :].bitcast(FP8X4), scales=w_scales[:, g, :], in_=grouped[g][:]
+                )
 
-        for group, half in half_groups[:LEAD]:
-            prepare(group, half)
-        rot = const.tile([P, BATCH, PAIRS, 2, 2], F32)
-        nc.scalar.activation(out=rot[:], in_=angle[:], func=ACT.Sin)
+        def multiply(i, b):
+            w_codes, w_scales = operands[i]
+            acc = acc_psum.tile([P, GROUP_COLS], F32, tag="acc")
+            for g in range(PASSES):
+                nc.tensor.matmul_mx(
+                    out=acc[:],
+                    lhsT=x_codes[:, g, P * b : P * b + P].bitcast(FP8X4),
+                    lhsT_scale=x_scales[:, g, P * b : P * b + P],
+                    rhs=w_codes[:, g, :].bitcast(FP8X4),
+                    rhs_scale=w_scales[:, g, :],
+                    start=(g == 0),
+                    stop=(g == PASSES - 1),
+                )
+            return acc
 
-        for step in range(len(units) // 2):
-            for group, half in half_groups[step + LEAD : step + LEAD + 1]:
-                prepare(group, half)
-            pair = units[2 * step : 2 * step + 2]
-            accs = [multiply(b, *operands[group]) for group, b in pair]
-            products = [
-                multiply_by_table(b, acc) if group[0] != 2 else None for (group, b), acc in zip(pair, accs)
-            ]
-            for (group, b), acc, planes in zip(pair, accs, products):
-                result = results.tile([P, GROUP_COLS], F32, tag="result")
-                if planes is None:
-                    nc.scalar.copy(out=result[:], in_=acc[:])
-                else:
-                    nc.gpsimd.tensor_tensor(
-                        out=result[:],
-                        in0=planes[:, 0].rearrange("s h n e -> s (h n e)"),
-                        in1=planes[:, 1].rearrange("s h n e -> s (h n e)"),
-                        op=ALU.add,
-                    )
-                store(group, b, result)
+        def rotate(i, b, acc, result):
+            which, c = groups[i]
+            products = work.tile([P, 2, GROUP_COLS], F32, tag="products")
+            phase = (c * GROUP_COLS // 2) % PAIRS
+            shape = [P, WHOLE_HEADS, PAIRS, 2, 2]
+            nc.vector.tensor_tensor(
+                out=products[:, :, :WHOLE].rearrange("s w (h n e) -> s h n w e", h=WHOLE_HEADS, e=2),
+                in0=acc[:, :WHOLE].rearrange("s (h n w) -> s h n w", h=WHOLE_HEADS, w=2).unsqueeze(4).to_broadcast(shape),
+                in1=rot[:, b, phase : phase + PAIRS].unsqueeze(1).to_broadcast(shape),
+                op=ALU.mult,
+            )
+            nc.vector.tensor_tensor(
+                out=products[:, :, WHOLE:].rearrange("s w (n e) -> s n w e", e=2),
+                in0=acc[:, WHOLE:].rearrange("s (n w) -> s n w", w=2).unsqueeze(3).to_broadcast([P, REST_PAIRS, 2, 2]),
+                in1=rot[:, b, phase : phase + REST_PAIRS],
+                op=ALU.mult,
+            )
+            nc.gpsimd.tensor_tensor(out=result, in0=products[:, 0, :], in1=products[:, 1, :], op=ALU.add)
+
+        result_tiles = {}
+
+        def finish(i, b, acc):
+            which, c = groups[i]
+            if c == 0:
+                result_row = results.tile([P, OUT_COLS], F32, tag="result_%d_%d" % (which, b))
+                result_tiles[(which, b)] = result_row
+            result = result_tiles[(which, b)]
+            columns = result[:, GROUP_COLS * c : GROUP_COLS * (c + 1)]
+            if which == 2:
+                nc.scalar.copy(out=columns, in_=acc[:])
+            else:
+                rotate(i, b, acc, columns)
+            h0 = GROUP_COLS * c // HEAD_DIM
+            h1 = GROUP_COLS * (c + 1) // HEAD_DIM
+            nc.sync.dma_start(
+                out=outputs[which][b, h0:h1].rearrange("h s d -> s h d"),
+                in_=result[:, HEAD_DIM * h0 : HEAD_DIM * h1].rearrange("s (h d) -> s h d", d=HEAD_DIM),
+            )
+
+        by_pass = [(g, half) for g in range(PASSES) for half in range(2)]
+        by_arrival = [(g, half) for half in range(2) for g in range(PASSES)]
+
+        quantise_x(0, flip_x(0))
+        prepare(0, by_arrival, 2)
+        for b in range(1, BATCH):
+            quantise_x(b, flip_x(b))
+        rot = const.tile([P, BATCH, 2 * PAIRS, 2, 2], F32)
+        nc.scalar.activation(
+            out=rot[:].rearrange("s b (r n) i e -> s b r (n i e)", r=2),
+            in_=angle[:].rearrange("s b n i e -> s b (n i e)").unsqueeze(2).to_broadcast([P, BATCH, 2, 4 * PAIRS]),
+            func=ACT.Sin,
+        )
+
+        for i in range(last + 1):
+            plain = groups[i][0] == 2
+            if 0 < i < last:
+                prepare(i + 1, by_pass, 3 if plain else 1)
+            spreads = [(i + 2, t) for t in range(SPREAD_TILES)] if FIRST_SPREAD <= i + 2 <= last else []
+            for b in range(BATCH):
+                if spreads:
+                    spread_tile(*spreads.pop(0))
+                finish(i, b, multiply(i, b))
+            if i == 0:
+                prepare(1, by_arrival, 2)

@@ -29,7 +29,6 @@ TILES = GROUP_COLS // P
 GROUPS_PER_OUTPUT = OUT_COLS // GROUP_COLS
 WHOLE_HEADS = GROUP_COLS // HEAD_DIM
 WHOLE = WHOLE_HEADS * HEAD_DIM
-REST_PAIRS = (GROUP_COLS - WHOLE) // 2
 FIRST_SPREAD = 3
 SPREAD_TILES = 3
 
@@ -75,14 +74,14 @@ def rotation_arguments(nc, const, coords_sb):
         out=magnitude[:], in0=reduced[:], scalar=-1.0, in1=reduced[:], op0=ALU.mult, op1=ALU.max
     )
 
-    angle = const.tile([P, BATCH, PAIRS, 2, 2], F32)
-    for i in range(2):
+    angle = const.tile([P, 2, BATCH, PAIRS, 2], F32)
+    for e in range(2):
         nc.vector.tensor_scalar(
-            out=angle[:, :, :, i, i], in0=magnitude[:], scalar1=-1.0, scalar2=0.5 * math.pi,
+            out=angle[:, 0, :, :, e], in0=magnitude[:], scalar1=-1.0, scalar2=0.5 * math.pi,
             op0=ALU.mult, op1=ALU.add,
         )
-    nc.vector.tensor_copy(out=angle[:, :, :, 0, 1], in_=reduced[:])
-    nc.vector.tensor_scalar(out=angle[:, :, :, 1, 0], in0=reduced[:], scalar1=-1.0, scalar2=None, op0=ALU.mult)
+    nc.vector.tensor_copy(out=angle[:, 1, :, :, 0], in_=reduced[:])
+    nc.vector.tensor_scalar(out=angle[:, 1, :, :, 1], in0=reduced[:], scalar1=-1.0, scalar2=None, op0=ALU.mult)
     return angle
 
 
@@ -234,21 +233,30 @@ def tile_ropeattention_pa_kernel(tc, x, coords, W_qkv, out_0, out_1, out_2):
         def rotate(i, b, acc, result):
             which, c = groups[i]
             products = work.tile([P, 2, GROUP_COLS], F32, tag="products")
-            phase = (c * GROUP_COLS // 2) % PAIRS
-            shape = [P, WHOLE_HEADS, PAIRS, 2, 2]
+            phase = c * GROUP_COLS % HEAD_DIM
+            shape = [P, WHOLE_HEADS, HEAD_DIM]
+            for plane in range(2):
+                table = rot[:, plane, b, phase : phase + HEAD_DIM]
+                nc.vector.tensor_tensor(
+                    out=products[:, plane, :WHOLE].rearrange("s (h d) -> s h d", h=WHOLE_HEADS),
+                    in0=acc[:, :WHOLE].rearrange("s (h d) -> s h d", h=WHOLE_HEADS),
+                    in1=table.unsqueeze(1).to_broadcast(shape),
+                    op=ALU.mult,
+                )
+            rest = GROUP_COLS - WHOLE
             nc.vector.tensor_tensor(
-                out=products[:, :, :WHOLE].rearrange("s w (h n e) -> s h n w e", h=WHOLE_HEADS, e=2),
-                in0=acc[:, :WHOLE].rearrange("s (h n w) -> s h n w", h=WHOLE_HEADS, w=2).unsqueeze(4).to_broadcast(shape),
-                in1=rot[:, b, phase : phase + PAIRS].unsqueeze(1).to_broadcast(shape),
+                out=products[:, :, WHOLE:],
+                in0=acc[:, WHOLE:].unsqueeze(1).to_broadcast([P, 2, rest]),
+                in1=rot[:, :, b, phase : phase + rest],
                 op=ALU.mult,
             )
-            nc.vector.tensor_tensor(
-                out=products[:, :, WHOLE:].rearrange("s w (n e) -> s n w e", e=2),
-                in0=acc[:, WHOLE:].rearrange("s (n w) -> s n w", w=2).unsqueeze(3).to_broadcast([P, REST_PAIRS, 2, 2]),
-                in1=rot[:, b, phase : phase + REST_PAIRS],
-                op=ALU.mult,
+            pairs = "s (n w) -> s n w"
+            nc.gpsimd.tensor_tensor(
+                out=result.rearrange(pairs, w=2),
+                in0=products[:, 0, :].rearrange(pairs, w=2),
+                in1=products[:, 1, :].rearrange(pairs, w=2)[:, :, ::-1],
+                op=ALU.add,
             )
-            nc.gpsimd.tensor_tensor(out=result, in0=products[:, 0, :], in1=products[:, 1, :], op=ALU.add)
 
         result_tiles = {}
 
@@ -277,10 +285,10 @@ def tile_ropeattention_pa_kernel(tc, x, coords, W_qkv, out_0, out_1, out_2):
         prepare(0, by_arrival, 2)
         for b in range(1, BATCH):
             quantise_x(b, flip_x(b))
-        rot = const.tile([P, BATCH, 2 * PAIRS, 2, 2], F32)
+        rot = const.tile([P, 2, BATCH, 2 * HEAD_DIM], F32)
         nc.scalar.activation(
-            out=rot[:].rearrange("s b (r n) i e -> s b r (n i e)", r=2),
-            in_=angle[:].rearrange("s b n i e -> s b (n i e)").unsqueeze(2).to_broadcast([P, BATCH, 2, 4 * PAIRS]),
+            out=rot[:].rearrange("s i b (r d) -> s (i b) r d", r=2),
+            in_=angle[:].rearrange("s i b n e -> s (i b) (n e)").unsqueeze(2).to_broadcast([P, 2 * BATCH, 2, HEAD_DIM]),
             func=ACT.Sin,
         )
 

@@ -27,8 +27,7 @@ OUT_COLS = HEADS * HEAD_DIM
 GROUP_COLS = 512
 TILES = GROUP_COLS // P
 GROUPS_PER_OUTPUT = OUT_COLS // GROUP_COLS
-WHOLE_HEADS = GROUP_COLS // HEAD_DIM
-WHOLE = WHOLE_HEADS * HEAD_DIM
+TABLE_HEADS = 6
 FIRST_SPREAD = 3
 SPREAD_TILES = 3
 
@@ -88,16 +87,15 @@ def rotation_arguments(nc, const, coords_sb):
 def tile_ropeattention_pa_kernel(tc, x, coords, W_qkv, out_0, out_1, out_2):
     nc = tc.nc
     outputs = (out_0, out_1, out_2)
-    groups = [(which, c) for c in range(GROUPS_PER_OUTPUT) for which in range(3)]
+    groups = [(which, c) for c in range(GROUPS_PER_OUTPUT) for which in (0, 2, 1)]
     last = len(groups) - 1
 
     with ExitStack() as ctx:
         const = ctx.enter_context(tc.tile_pool(name="const", bufs=1))
-        rows_pool = ctx.enter_context(tc.tile_pool(name="rows_pool", bufs=11))
-        spread_pool = ctx.enter_context(tc.tile_pool(name="spread_pool", bufs=5))
-        stage_x = ctx.enter_context(tc.tile_pool(name="stage_x", bufs=2))
-        stage = ctx.enter_context(tc.tile_pool(name="stage", bufs=5))
-        packed = ctx.enter_context(tc.tile_pool(name="packed", bufs=2))
+        rows_pool = ctx.enter_context(tc.tile_pool(name="rows_pool", bufs=9))
+        spread_pool = ctx.enter_context(tc.tile_pool(name="spread_pool", bufs=3))
+        stage = ctx.enter_context(tc.tile_pool(name="stage", bufs=2))
+        packed = ctx.enter_context(tc.tile_pool(name="packed", bufs=3))
         work = ctx.enter_context(tc.tile_pool(name="work", bufs=3))
         results = ctx.enter_context(tc.tile_pool(name="results", bufs=1))
         flip_psum = ctx.enter_context(tc.psum_pool(name="flip_psum", bufs=4))
@@ -144,40 +142,42 @@ def tile_ropeattention_pa_kernel(tc, x, coords, W_qkv, out_0, out_1, out_2):
         make_identity(nc, identity[:])
         angle = rotation_arguments(nc, const, coords_sb)
 
-        x_codes = const.tile([P, PASSES, BATCH * P], U32, align_bytes=64)
-        x_scales = const.tile([P, PASSES, BATCH * P], U8, align_bytes=64)
+        x_codes = const.tile([P, BATCH, PASSES, P], U32, align_bytes=64)
+        x_scales = const.tile([P, BATCH, PASSES, P], U8, align_bytes=64)
+        x_grouped = stage.tile([P, BATCH, PASSES, 4 * P], BF16, tag="grouped", align_bytes=64)
 
         def every_second(words, g, u):
             return words[:, PASS_WORDS * g + u : PASS_WORDS * (g + 1) : 2]
 
         def flip_x(b):
             words = x_rows[b // 2][:].bitcast(F32)[:, b % 2, :]
-            grouped = stage_x.tile([P, PASSES, 4 * P], BF16, tag="grouped_x", align_bytes=64)
             for g0, g1 in ((0, 2), (2, 3)):
                 flipped = flip_psum.tile([P, g1 - g0, 2, P], F32, tag="flipped")
                 for g in range(g0, g1):
                     for u in range(2):
                         nc.tensor.transpose(flipped[:, g - g0, u, :], every_second(words, g, u), identity[:])
                 nc.scalar.copy(
-                    out=grouped[:, g0:g1, :].bitcast(F32).rearrange("q g (c u) -> q g c u", u=2),
+                    out=x_grouped[:, b, g0:g1, :].bitcast(F32).rearrange("q g (c u) -> q g c u", u=2),
                     in_=flipped[:].rearrange("q g u c -> q g c u"),
                 )
-            return grouped
 
-        def quantise_x(b, grouped):
-            for g in range(PASSES):
+        def quantise_x(first, widths):
+            codes = x_codes[:].rearrange("q b g c -> q (b g c)")
+            scales = x_scales[:].rearrange("q b g c -> q (b g c)")
+            grouped = x_grouped[:].rearrange("q b g w -> q (b g w)")
+            for n in widths:
+                lo, hi = P * first, P * (first + n)
                 nc.vector.quantize_mx(
-                    out=x_codes[:, g, P * b : P * b + P].bitcast(FP8X4),
-                    scales=x_scales[:, g, P * b : P * b + P],
-                    in_=grouped[:, g, :],
+                    out=codes[:, lo:hi].bitcast(FP8X4), scales=scales[:, lo:hi], in_=grouped[:, 4 * lo : 4 * hi]
                 )
+                first += n
 
         spread = {}
 
-        def spread_tile(i, t):
+        def spread_tile(copy, i, t):
             tile = spread_pool.tile([P, PASSES, 2, P], F32, tag="spread")
             words = w_rows[(i, t // 2)][:].bitcast(F32)[:, t % 2, :]
-            nc.scalar.copy(out=tile[:], in_=words.rearrange("r (g q u) -> r g u q", g=PASSES, u=2))
+            copy(out=tile[:], in_=words.rearrange("r (g q u) -> r g u q", g=PASSES, u=2))
             spread[(i, t)] = tile
 
         def flip_bank(i, g, half):
@@ -191,38 +191,35 @@ def tile_ropeattention_pa_kernel(tc, x, coords, W_qkv, out_0, out_1, out_2):
                     nc.tensor.transpose(flipped[:, u, P * t : P * t + P], words, identity[:])
             return flipped
 
-        def empty_bank(copy, flipped, grouped, half):
-            copy(
-                out=grouped[:].bitcast(F32)[:, 512 * half : 512 * half + 512].rearrange("q (c u) -> q c u", u=2),
-                in_=flipped[:].rearrange("q u c -> q c u"),
-            )
-
         operands = {}
 
-        def prepare(i, order, on_vector):
-            w_codes = packed.tile([P, PASSES, GROUP_COLS], U32, tag="w_codes", align_bytes=64)
-            w_scales = packed.tile([P, PASSES, GROUP_COLS], U8, tag="w_scales", align_bytes=64)
-            operands[i] = (w_codes, w_scales)
-            grouped = []
-            for g in range(PASSES):
-                grouped_g = stage.tile([P, 4 * GROUP_COLS], BF16, tag="grouped", align_bytes=64)
-                grouped.append(grouped_g)
-            for n, (g, half) in enumerate(order):
-                copy = nc.vector.tensor_copy if n >= len(order) - on_vector else nc.scalar.copy
-                empty_bank(copy, flip_bank(i, g, half), grouped[g], half)
-            for g in range(PASSES):
+        def prepare(i, banks, on_vector, parts):
+            if i not in operands:
+                w_codes = packed.tile([P, PASSES, GROUP_COLS], U32, tag="w_codes", align_bytes=64)
+                w_scales = packed.tile([P, PASSES, GROUP_COLS], U8, tag="w_scales", align_bytes=64)
+                grouped = stage.tile([P, PASSES, 4 * GROUP_COLS], BF16, tag="grouped", align_bytes=64)
+                operands[i] = (w_codes, w_scales, grouped)
+            w_codes, w_scales, grouped = operands[i]
+            for n, (g, half) in enumerate(banks):
+                copy = nc.vector.tensor_copy if n >= len(banks) - on_vector else nc.scalar.copy
+                flipped = flip_bank(i, g, half)
+                words = grouped[:, g, :].bitcast(F32)[:, 512 * half : 512 * half + 512]
+                copy(out=words.rearrange("q (c u) -> q c u", u=2), in_=flipped[:].rearrange("q u c -> q c u"))
+            for g0, g1 in parts:
                 nc.vector.quantize_mx(
-                    out=w_codes[:, g, :].bitcast(FP8X4), scales=w_scales[:, g, :], in_=grouped[g][:]
+                    out=w_codes[:, g0:g1, :].rearrange("q g c -> q (g c)").bitcast(FP8X4),
+                    scales=w_scales[:, g0:g1, :].rearrange("q g c -> q (g c)"),
+                    in_=grouped[:, g0:g1, :].rearrange("q g w -> q (g w)"),
                 )
 
         def multiply(i, b):
-            w_codes, w_scales = operands[i]
+            w_codes, w_scales, grouped = operands[i]
             acc = acc_psum.tile([P, GROUP_COLS], F32, tag="acc")
             for g in range(PASSES):
                 nc.tensor.matmul_mx(
                     out=acc[:],
-                    lhsT=x_codes[:, g, P * b : P * b + P].bitcast(FP8X4),
-                    lhsT_scale=x_scales[:, g, P * b : P * b + P],
+                    lhsT=x_codes[:, b, g, :].bitcast(FP8X4),
+                    lhsT_scale=x_scales[:, b, g, :],
                     rhs=w_codes[:, g, :].bitcast(FP8X4),
                     rhs_scale=w_scales[:, g, :],
                     start=(g == 0),
@@ -230,76 +227,106 @@ def tile_ropeattention_pa_kernel(tc, x, coords, W_qkv, out_0, out_1, out_2):
                 )
             return acc
 
-        def rotate(i, b, acc, result):
+        result_tiles = {}
+
+        def columns_of(i, b):
+            which, c = groups[i]
+            if c == 0:
+                result_row = results.tile([P, OUT_COLS], F32, tag="result_%d_%d" % (which, b))
+                result_tiles[(which, b)] = result_row
+            return result_tiles[(which, b)][:, GROUP_COLS * c : GROUP_COLS * (c + 1)]
+
+        def times_table(i, b, acc):
             which, c = groups[i]
             products = work.tile([P, 2, GROUP_COLS], F32, tag="products")
             phase = c * GROUP_COLS % HEAD_DIM
-            shape = [P, WHOLE_HEADS, HEAD_DIM]
-            for plane in range(2):
-                table = rot[:, plane, b, phase : phase + HEAD_DIM]
-                nc.vector.tensor_tensor(
-                    out=products[:, plane, :WHOLE].rearrange("s (h d) -> s h d", h=WHOLE_HEADS),
-                    in0=acc[:, :WHOLE].rearrange("s (h d) -> s h d", h=WHOLE_HEADS),
-                    in1=table.unsqueeze(1).to_broadcast(shape),
-                    op=ALU.mult,
-                )
-            rest = GROUP_COLS - WHOLE
             nc.vector.tensor_tensor(
-                out=products[:, :, WHOLE:],
-                in0=acc[:, WHOLE:].unsqueeze(1).to_broadcast([P, 2, rest]),
-                in1=rot[:, :, b, phase : phase + rest],
+                out=products[:],
+                in0=acc[:].unsqueeze(1).to_broadcast([P, 2, GROUP_COLS]),
+                in1=rot[:, :, b, phase : phase + GROUP_COLS],
                 op=ALU.mult,
             )
+            return products
+
+        def add_planes(engine, i, b, products):
             pairs = "s (n w) -> s n w"
-            nc.gpsimd.tensor_tensor(
-                out=result.rearrange(pairs, w=2),
+            engine.tensor_tensor(
+                out=columns_of(i, b).rearrange(pairs, w=2),
                 in0=products[:, 0, :].rearrange(pairs, w=2),
                 in1=products[:, 1, :].rearrange(pairs, w=2)[:, :, ::-1],
                 op=ALU.add,
             )
 
-        result_tiles = {}
-
-        def finish(i, b, acc):
+        def store(i, b):
             which, c = groups[i]
-            if c == 0:
-                result_row = results.tile([P, OUT_COLS], F32, tag="result_%d_%d" % (which, b))
-                result_tiles[(which, b)] = result_row
-            result = result_tiles[(which, b)]
-            columns = result[:, GROUP_COLS * c : GROUP_COLS * (c + 1)]
-            if which == 2:
-                nc.scalar.copy(out=columns, in_=acc[:])
-            else:
-                rotate(i, b, acc, columns)
             h0 = GROUP_COLS * c // HEAD_DIM
             h1 = GROUP_COLS * (c + 1) // HEAD_DIM
             nc.sync.dma_start(
                 out=outputs[which][b, h0:h1].rearrange("h s d -> s h d"),
-                in_=result[:, HEAD_DIM * h0 : HEAD_DIM * h1].rearrange("s (h d) -> s h d", d=HEAD_DIM),
+                in_=result_tiles[(which, b)][:, HEAD_DIM * h0 : HEAD_DIM * h1].rearrange("s (h d) -> s h d", d=HEAD_DIM),
+            )
+
+        rot = const.tile([P, 2, BATCH, TABLE_HEADS * HEAD_DIM], F32)
+
+        def fill_table(b):
+            nc.scalar.activation(
+                out=rot[:, :, b, :].rearrange("s i (h d) -> s i h d", d=HEAD_DIM),
+                in_=angle[:, :, b].rearrange("s i n e -> s i (n e)").unsqueeze(2).to_broadcast([P, 2, TABLE_HEADS, HEAD_DIM]),
+                func=ACT.Sin,
             )
 
         by_pass = [(g, half) for g in range(PASSES) for half in range(2)]
         by_arrival = [(g, half) for half in range(2) for g in range(PASSES)]
 
-        quantise_x(0, flip_x(0))
-        prepare(0, by_arrival, 2)
+        flip_x(0)
+        quantise_x(0, (2, 1))
+        prepare(0, by_arrival, 0, ((0, 2), (2, 3)))
         for b in range(1, BATCH):
-            quantise_x(b, flip_x(b))
-        rot = const.tile([P, 2, BATCH, 2 * HEAD_DIM], F32)
-        nc.scalar.activation(
-            out=rot[:].rearrange("s i b (r d) -> s (i b) r d", r=2),
-            in_=angle[:].rearrange("s i b n e -> s (i b) (n e)").unsqueeze(2).to_broadcast([P, 2 * BATCH, 2, HEAD_DIM]),
-            func=ACT.Sin,
-        )
-
-        for i in range(last + 1):
-            plain = groups[i][0] == 2
-            if 0 < i < last:
-                prepare(i + 1, by_pass, 3 if plain else 1)
-            spreads = [(i + 2, t) for t in range(SPREAD_TILES)] if FIRST_SPREAD <= i + 2 <= last else []
-            for b in range(BATCH):
-                if spreads:
-                    spread_tile(*spreads.pop(0))
-                finish(i, b, multiply(i, b))
-            if i == 0:
-                prepare(1, by_arrival, 2)
+            flip_x(b)
+        quantise_x(3, (8, 1))
+        for b in range(BATCH):
+            fill_table(b)
+        steps = []
+        for c in range(GROUPS_PER_OUTPUT):
+            q, v, k = 3 * c, 3 * c + 1, 3 * c + 2
+            if c == 0:
+                steps.append(((), [(q, 0), (q, 1), (q, 2), (q, 3)]))
+                steps.append(((v, k), [(v, 0), (v, 1), (k, 0), (k, 1)]))
+                steps.append(((k + 1,), [(v, 2), (k, 2), (k, 3), (v, 3)]))
+            else:
+                steps.append(((v,), [(q, 0), (q, 1), (v, 0), (q, 2)]))
+                steps.append(((k,), [(q, 3), (v, 1), (k, 0), (k, 1)]))
+                steps.append(((k + 1,) if k < last else (), [(v, 2), (k, 2), (k, 3), (v, 3)]))
+        prep_step = {}
+        for n, (prep, units) in enumerate(steps):
+            for j in prep:
+                prep_step[j] = n
+        vs = {}
+        ss = {}
+        for j in range(4, len(groups)):
+            for t in range(1):
+                vs.setdefault(prep_step[j] - 1, []).append((j, t))
+        for j in range(4, len(groups)):
+            for t in range(1, 1 + 1):
+                ss.setdefault(prep_step[j] - 1, []).append((j, t))
+        for n, (prep, units) in enumerate(steps):
+            for s in vs.get(n, []):
+                spread_tile(nc.vector.tensor_copy, *s)
+            for j in prep:
+                prepare(j, by_pass if j > 2 else by_arrival, 0, ((0, 2), (2, 3)))
+            for p in range(0, BATCH, 2):
+                pair = units[p : p + 2]
+                accs = [multiply(i, b) for i, b in pair]
+                products = {}
+                for k, (i, b) in enumerate(pair):
+                    if groups[i][0] == 2:
+                        nc.scalar.copy(out=columns_of(i, b), in_=accs[k][:])
+                    else:
+                        products[(i, b)] = times_table(i, b, accs[k])
+                for k, (i, b) in enumerate(pair):
+                    if groups[i][0] != 2:
+                        add_planes(nc.vector if False else nc.gpsimd, i, b, products[(i, b)])
+                    store(i, b)
+                if p == 0:
+                    for s in ss.get(n, []):
+                        spread_tile(nc.scalar.copy, *s)

@@ -40,17 +40,26 @@ ROUND_MAGIC = 12582912.0
 PI_BELOW = 3.1415925
 
 
-def rotation_arguments(nc, const, coords_sb):
-    theta = const.tile([P, BATCH, PAIRS], F32)
-    theta_by_freq = theta[:].rearrange("s b (a j) -> s (b a) j", j=FREQS)
+def frequencies(nc, const):
+    ones = const.tile([P, 1], F32)
+    nc.vector.memset(ones[:], 1.0)
+    freqs = const.tile([P, FREQS], F32)
     for j in range(FREQS):
         nc.vector.tensor_scalar(
-            out=theta_by_freq[:, :, j],
-            in0=coords_sb[:].rearrange("s b a -> s (b a)"),
-            scalar1=10000.0 ** (-j / FREQS),
-            scalar2=None,
-            op0=ALU.mult,
+            out=freqs[:, j : j + 1], in0=ones[:], scalar1=10000.0 ** (-j / FREQS), scalar2=None, op0=ALU.mult
         )
+    return freqs
+
+
+def rotation_arguments(nc, const, coords_sb, freqs):
+    theta = const.tile([P, BATCH, PAIRS], F32)
+    axes = [P, BATCH * 3, FREQS]
+    nc.vector.tensor_tensor(
+        out=theta[:].rearrange("s b (a j) -> s (b a) j", j=FREQS),
+        in0=coords_sb[:].rearrange("s b a -> s (b a)").unsqueeze(2).to_broadcast(axes),
+        in1=freqs[:].unsqueeze(1).to_broadcast(axes),
+        op=ALU.mult,
+    )
 
     turns = const.tile([P, BATCH, PAIRS], F32)
     nc.vector.tensor_scalar(
@@ -68,17 +77,21 @@ def rotation_arguments(nc, const, coords_sb):
     nc.vector.tensor_scalar(
         out=reduced[:], in0=reduced[:], scalar1=-PI_BELOW, scalar2=PI_BELOW, op0=ALU.max, op1=ALU.min
     )
+    return reduced
+
+
+def rotation_angles(nc, const, reduced):
     magnitude = const.tile([P, BATCH, PAIRS], F32)
     nc.vector.scalar_tensor_tensor(
         out=magnitude[:], in0=reduced[:], scalar=-1.0, in1=reduced[:], op0=ALU.mult, op1=ALU.max
     )
 
     angle = const.tile([P, 2, BATCH, PAIRS, 2], F32)
-    for e in range(2):
-        nc.vector.tensor_scalar(
-            out=angle[:, 0, :, :, e], in0=magnitude[:], scalar1=-1.0, scalar2=0.5 * math.pi,
-            op0=ALU.mult, op1=ALU.add,
-        )
+    nc.vector.tensor_scalar(
+        out=angle[:, 0],
+        in0=magnitude[:].unsqueeze(3).to_broadcast([P, BATCH, PAIRS, 2]),
+        scalar1=-1.0, scalar2=0.5 * math.pi, op0=ALU.mult, op1=ALU.add,
+    )
     nc.vector.tensor_copy(out=angle[:, 1, :, :, 0], in_=reduced[:])
     nc.vector.tensor_scalar(out=angle[:, 1, :, :, 1], in0=reduced[:], scalar1=-1.0, scalar2=None, op0=ALU.mult)
     return angle
@@ -134,13 +147,13 @@ def tile_ropeattention_pa_kernel(tc, x, coords, W_qkv, out_0, out_1, out_2):
         for i in range(1, last + 1):
             load_group(i, 2)
 
+        freqs = frequencies(nc, const)
         warm = const.tile([P, 1], F32)
         nc.vector.memset(warm[:], 0.0)
         nc.scalar.activation(out=warm[:], in_=warm[:], func=ACT.Sin)
 
         identity = const.tile([P, P], F32)
         make_identity(nc, identity[:])
-        angle = rotation_arguments(nc, const, coords_sb)
 
         x_codes = const.tile([P, BATCH, PASSES, P], U32, align_bytes=64)
         x_scales = const.tile([P, BATCH, PASSES, P], U8, align_bytes=64)
@@ -278,55 +291,64 @@ def tile_ropeattention_pa_kernel(tc, x, coords, W_qkv, out_0, out_1, out_2):
         by_pass = [(g, half) for g in range(PASSES) for half in range(2)]
         by_arrival = [(g, half) for half in range(2) for g in range(PASSES)]
 
+        reduced = rotation_arguments(nc, const, coords_sb, freqs)
         flip_x(0)
         quantise_x(0, (2, 1))
         prepare(0, by_arrival, 0, ((0, 2), (2, 3)))
+        angle = rotation_angles(nc, const, reduced)
         for b in range(1, BATCH):
             flip_x(b)
+        fill_table(0)
         quantise_x(3, (8, 1))
-        for b in range(BATCH):
-            fill_table(b)
-        steps = []
+        slots = []
         for c in range(GROUPS_PER_OUTPUT):
             q, v, k = 3 * c, 3 * c + 1, 3 * c + 2
             if c == 0:
-                steps.append(((), [(q, 0), (q, 1), (q, 2), (q, 3)]))
-                steps.append(((v, k), [(v, 0), (v, 1), (k, 0), (k, 1)]))
-                steps.append(((k + 1,), [(v, 2), (k, 2), (k, 3), (v, 3)]))
+                slots += [
+                    ((), [(q, 0)]),
+                    ((v,), [(q, 1), (q, 2), (q, 3)]),
+                    ((k,), [(v, 0), (v, 1)]),
+                    ((k + 1,), [(v, 2), (k, 0)]),
+                    ((), [(k, 1), (k, 2)]),
+                    ((k + 2,), [(k, 3), (v, 3)]),
+                ]
             else:
-                steps.append(((v,), [(q, 0), (q, 1), (v, 0), (q, 2)]))
-                steps.append(((k,), [(q, 3), (v, 1), (k, 0), (k, 1)]))
-                steps.append(((k + 1,) if k < last else (), [(v, 2), (k, 2), (k, 3), (v, 3)]))
-        prep_step = {}
-        for n, (prep, units) in enumerate(steps):
+                slots += [
+                    ((k,), [(q, 0), (q, 1)]),
+                    ((), [(v, 0), (q, 2)]),
+                    ((k + 1,) if k < last else (), [(q, 3), (v, 1)]),
+                    ((), [(k, 0), (k, 1)]),
+                    ((k + 2,) if k < last else (), [(v, 2), (k, 2)]),
+                    ((), [(k, 3), (v, 3)]),
+                ]
+        prep_slot = {}
+        for n, (prep, units) in enumerate(slots):
             for j in prep:
-                prep_step[j] = n
-        vs = {}
-        ss = {}
-        for j in range(4, len(groups)):
-            for t in range(1):
-                vs.setdefault(prep_step[j] - 1, []).append((j, t))
-        for j in range(4, len(groups)):
-            for t in range(1, 1 + 1):
-                ss.setdefault(prep_step[j] - 1, []).append((j, t))
-        for n, (prep, units) in enumerate(steps):
-            for s in vs.get(n, []):
-                spread_tile(nc.vector.tensor_copy, *s)
+                prep_slot[j] = n
+        spreads = ((1, nc.scalar.copy, 2, False),)
+        first_spread = 4
+        for n, (prep, units) in enumerate(slots):
+            for t, copy, ahead, before in spreads:
+                for j in range(first_spread, len(groups)):
+                    if before and prep_slot[j] == n + ahead:
+                        spread_tile(copy, j, t)
             for j in prep:
-                prepare(j, by_pass if j > 2 else by_arrival, 0, ((0, 2), (2, 3)))
-            for p in range(0, BATCH, 2):
-                pair = units[p : p + 2]
-                accs = [multiply(i, b) for i, b in pair]
-                products = {}
-                for k, (i, b) in enumerate(pair):
-                    if groups[i][0] == 2:
-                        nc.scalar.copy(out=columns_of(i, b), in_=accs[k][:])
-                    else:
-                        products[(i, b)] = times_table(i, b, accs[k])
-                for k, (i, b) in enumerate(pair):
-                    if groups[i][0] != 2:
-                        add_planes(nc.vector if False else nc.gpsimd, i, b, products[(i, b)])
-                    store(i, b)
-                if p == 0:
-                    for s in ss.get(n, []):
-                        spread_tile(nc.scalar.copy, *s)
+                prepare(j, by_pass, 0, ((0, 2), (2, 3)))
+            if n == 1:
+                for b in range(1, BATCH):
+                    fill_table(b)
+            accs = [multiply(i, b) for i, b in units]
+            products = {}
+            for k, (i, b) in enumerate(units):
+                if groups[i][0] == 2:
+                    nc.scalar.copy(out=columns_of(i, b), in_=accs[k][:])
+                else:
+                    products[(i, b)] = times_table(i, b, accs[k])
+            for k, (i, b) in enumerate(units):
+                if groups[i][0] != 2:
+                    add_planes(nc.vector if b == 3 else nc.gpsimd, i, b, products[(i, b)])
+                store(i, b)
+            for t, copy, ahead, before in spreads:
+                for j in range(first_spread, len(groups)):
+                    if not before and prep_slot[j] == n + ahead:
+                        spread_tile(copy, j, t)

@@ -105,10 +105,10 @@ def tile_ropeattention_pa_kernel(tc, x, coords, W_qkv, out_0, out_1, out_2):
 
     with ExitStack() as ctx:
         const = ctx.enter_context(tc.tile_pool(name="const", bufs=1))
-        rows_pool = ctx.enter_context(tc.tile_pool(name="rows_pool", bufs=9))
-        spread_pool = ctx.enter_context(tc.tile_pool(name="spread_pool", bufs=3))
+        rows_pool = ctx.enter_context(tc.tile_pool(name="rows_pool", bufs=8))
+        spread_pool = ctx.enter_context(tc.tile_pool(name="spread_pool", bufs=4))
         stage = ctx.enter_context(tc.tile_pool(name="stage", bufs=2))
-        packed = ctx.enter_context(tc.tile_pool(name="packed", bufs=3))
+        packed = ctx.enter_context(tc.tile_pool(name="packed", bufs=4))
         work = ctx.enter_context(tc.tile_pool(name="work", bufs=3))
         results = ctx.enter_context(tc.tile_pool(name="results", bufs=1))
         flip_psum = ctx.enter_context(tc.psum_pool(name="flip_psum", bufs=4))
@@ -225,6 +225,16 @@ def tile_ropeattention_pa_kernel(tc, x, coords, W_qkv, out_0, out_1, out_2):
                     in_=grouped[:, g0:g1, :].rearrange("q g w -> q (g w)"),
                 )
 
+        def quantise_half(i, half):
+            w_codes, w_scales, grouped = operands[i]
+            lo, hi = 256 * half, 256 * half + 256
+            for g in range(PASSES):
+                nc.vector.quantize_mx(
+                    out=w_codes[:, g, lo:hi].bitcast(FP8X4),
+                    scales=w_scales[:, g, lo:hi],
+                    in_=grouped[:, g, 4 * lo : 4 * hi],
+                )
+
         def multiply(i, b):
             w_codes, w_scales, grouped = operands[i]
             acc = acc_psum.tile([P, GROUP_COLS], F32, tag="acc")
@@ -281,11 +291,18 @@ def tile_ropeattention_pa_kernel(tc, x, coords, W_qkv, out_0, out_1, out_2):
 
         rot = const.tile([P, 2, BATCH, TABLE_HEADS * HEAD_DIM], F32)
 
-        def fill_table(b):
+        def fill_table():
             nc.scalar.activation(
-                out=rot[:, :, b, :].rearrange("s i (h d) -> s i h d", d=HEAD_DIM),
-                in_=angle[:, :, b].rearrange("s i n e -> s i (n e)").unsqueeze(2).to_broadcast([P, 2, TABLE_HEADS, HEAD_DIM]),
+                out=rot[:, :, :, :HEAD_DIM],
+                in_=angle[:].rearrange("s i b n e -> s i b (n e)"),
                 func=ACT.Sin,
+            )
+
+        def repeat_table(b):
+            shape = [P, 2, TABLE_HEADS - 1, HEAD_DIM]
+            nc.vector.tensor_copy(
+                out=rot[:, :, b, HEAD_DIM:].rearrange("s i (h d) -> s i h d", d=HEAD_DIM),
+                in_=rot[:, :, b, :HEAD_DIM].unsqueeze(2).to_broadcast(shape),
             )
 
         by_pass = [(g, half) for g in range(PASSES) for half in range(2)]
@@ -294,49 +311,43 @@ def tile_ropeattention_pa_kernel(tc, x, coords, W_qkv, out_0, out_1, out_2):
         reduced = rotation_arguments(nc, const, coords_sb, freqs)
         flip_x(0)
         quantise_x(0, (2, 1))
-        prepare(0, by_arrival, 0, ((0, 2), (2, 3)))
+        prepare(0, by_arrival[:3], 0, ())
+        quantise_half(0, 0)
+        prepare(0, by_arrival[3:], 0, ())
+        quantise_half(0, 1)
         angle = rotation_angles(nc, const, reduced)
-        for b in range(1, BATCH):
-            flip_x(b)
-        fill_table(0)
-        quantise_x(3, (8, 1))
-        slots = []
-        for c in range(GROUPS_PER_OUTPUT):
-            q, v, k = 3 * c, 3 * c + 1, 3 * c + 2
-            if c == 0:
-                slots += [
-                    ((), [(q, 0)]),
-                    ((v,), [(q, 1), (q, 2), (q, 3)]),
-                    ((k,), [(v, 0), (v, 1)]),
-                    ((k + 1,), [(v, 2), (k, 0)]),
-                    ((), [(k, 1), (k, 2)]),
-                    ((k + 2,), [(k, 3), (v, 3)]),
-                ]
-            else:
-                slots += [
-                    ((k,), [(q, 0), (q, 1)]),
-                    ((), [(v, 0), (q, 2)]),
-                    ((k + 1,) if k < last else (), [(q, 3), (v, 1)]),
-                    ((), [(k, 0), (k, 1)]),
-                    ((k + 2,) if k < last else (), [(v, 2), (k, 2)]),
-                    ((), [(k, 3), (v, 3)]),
-                ]
-        prep_slot = {}
+        flip_x(1)
+        fill_table()
+        repeat_table(0)
+        rotated = [(3 * c + w, b) for c in range(GROUPS_PER_OUTPUT) for w in (0, 2) for b in range(BATCH)]
+        plain = [(3 * c + 1, b) for c in range(GROUPS_PER_OUTPUT) for b in range(BATCH)]
+        units = []
+        while rotated or plain:
+            turn = plain if plain and (len(units) % 3 == 0 and len(units) >= 3 or not rotated) else rotated
+            units.append(turn.pop(0))
+        slot_units = [units[:1], units[1:4]] + [units[n : n + 2] for n in range(4, len(units), 2)]
+        first_slot = {}
+        for n, slot in enumerate(slot_units):
+            for i, b in slot:
+                first_slot.setdefault(i, n)
+        prep_slot = {last: first_slot[last] - 1}
+        for j in range(last - 1, 0, -1):
+            prep_slot[j] = max(1, min(first_slot[j] - 1, prep_slot[j + 1] - 1))
+        slots = [([j for j in range(1, last + 1) if prep_slot[j] == n], slot) for n, slot in enumerate(slot_units)]
+        plan = {j: [(1, nc.scalar.copy, 2, True)] for j in range(3, last + 1)}
         for n, (prep, units) in enumerate(slots):
-            for j in prep:
-                prep_slot[j] = n
-        spreads = ((1, nc.scalar.copy, 2, False),)
-        first_spread = 4
-        for n, (prep, units) in enumerate(slots):
-            for t, copy, ahead, before in spreads:
-                for j in range(first_spread, len(groups)):
+            if n == 1:
+                for b in range(2, BATCH):
+                    flip_x(b)
+                quantise_x(3, (8, 1))
+                for b in range(1, BATCH):
+                    repeat_table(b)
+            for j in plan:
+                for t, copy, ahead, before in plan[j]:
                     if before and prep_slot[j] == n + ahead:
                         spread_tile(copy, j, t)
             for j in prep:
                 prepare(j, by_pass, 0, ((0, 2), (2, 3)))
-            if n == 1:
-                for b in range(1, BATCH):
-                    fill_table(b)
             accs = [multiply(i, b) for i, b in units]
             products = {}
             for k, (i, b) in enumerate(units):
@@ -346,9 +357,9 @@ def tile_ropeattention_pa_kernel(tc, x, coords, W_qkv, out_0, out_1, out_2):
                     products[(i, b)] = times_table(i, b, accs[k])
             for k, (i, b) in enumerate(units):
                 if groups[i][0] != 2:
-                    add_planes(nc.vector if b == 3 else nc.gpsimd, i, b, products[(i, b)])
+                    add_planes(nc.vector if False else nc.gpsimd, i, b, products[(i, b)])
                 store(i, b)
-            for t, copy, ahead, before in spreads:
-                for j in range(first_spread, len(groups)):
+            for j in plan:
+                for t, copy, ahead, before in plan[j]:
                     if not before and prep_slot[j] == n + ahead:
                         spread_tile(copy, j, t)

@@ -14,6 +14,10 @@ ACT = mybir.ActivationFunctionType
 
 P = 128
 BATCH = 4
+TOKENS = 128
+RUN = 2
+PAIR_BATCHES = 2
+SLOTS = 4
 FEATURES = 1536
 HEADS = 16
 HEAD_DIM = 96
@@ -25,11 +29,8 @@ PASS_WORDS = K_PASS // 2
 OUT_COLS = HEADS * HEAD_DIM
 
 GROUP_COLS = 512
-TILES = GROUP_COLS // P
-GROUPS_PER_OUTPUT = OUT_COLS // GROUP_COLS
+CHUNKS = OUT_COLS // GROUP_COLS
 TABLE_HEADS = 6
-FIRST_SPREAD = 3
-SPREAD_TILES = 3
 
 FLOPS = 2 * BATCH * P * FEATURES * 3 * OUT_COLS
 
@@ -41,32 +42,34 @@ PI_BELOW = 3.1415925
 
 
 def frequencies(nc, const):
-    ones = const.tile([P, 1], F32)
-    nc.vector.memset(ones[:], 1.0)
     freqs = const.tile([P, FREQS], F32)
-    for j in range(FREQS):
+    nc.vector.memset(freqs[:, 0:1], 1.0)
+    n = 1
+    while n < FREQS:
         nc.vector.tensor_scalar(
-            out=freqs[:, j : j + 1], in0=ones[:], scalar1=10000.0 ** (-j / FREQS), scalar2=None, op0=ALU.mult
+            out=freqs[:, n : 2 * n], in0=freqs[:, 0:n], scalar1=10000.0 ** (-n / FREQS), scalar2=None, op0=ALU.mult
         )
+        n *= 2
     return freqs
 
 
 def rotation_arguments(nc, const, coords_sb, freqs):
-    theta = const.tile([P, BATCH, PAIRS], F32)
-    axes = [P, BATCH * 3, FREQS]
-    nc.vector.tensor_tensor(
-        out=theta[:].rearrange("s b (a j) -> s (b a) j", j=FREQS),
-        in0=coords_sb[:].rearrange("s b a -> s (b a)").unsqueeze(2).to_broadcast(axes),
-        in1=freqs[:].unsqueeze(1).to_broadcast(axes),
-        op=ALU.mult,
-    )
+    theta = const.tile([P, SLOTS, PAIRS], F32)
+    axes = [P, RUN * 3, FREQS]
+    for pair in range(SLOTS // RUN):
+        nc.vector.tensor_tensor(
+            out=theta[:, RUN * pair : RUN * pair + RUN, :].rearrange("p r (a j) -> p (r a) j", j=FREQS),
+            in0=coords_sb[:, pair, : RUN * 3].unsqueeze(2).to_broadcast(axes),
+            in1=freqs[:].unsqueeze(1).to_broadcast(axes),
+            op=ALU.mult,
+        )
 
-    turns = const.tile([P, BATCH, PAIRS], F32)
+    turns = const.tile([P, SLOTS, PAIRS], F32)
     nc.vector.tensor_scalar(
         out=turns[:], in0=theta[:], scalar1=0.5 / math.pi, scalar2=ROUND_MAGIC, op0=ALU.mult, op1=ALU.add
     )
     nc.vector.tensor_scalar(out=turns[:], in0=turns[:], scalar1=ROUND_MAGIC, scalar2=None, op0=ALU.subtract)
-    reduced = const.tile([P, BATCH, PAIRS], F32)
+    reduced = const.tile([P, SLOTS, PAIRS], F32)
     nc.vector.scalar_tensor_tensor(
         out=reduced[:], in0=turns[:], scalar=-TURN_HI, in1=theta[:], op0=ALU.mult, op1=ALU.add
     )
@@ -81,71 +84,79 @@ def rotation_arguments(nc, const, coords_sb, freqs):
 
 
 def rotation_angles(nc, const, reduced):
-    magnitude = const.tile([P, BATCH, PAIRS], F32)
+    magnitude = const.tile([P, SLOTS, PAIRS], F32)
     nc.vector.scalar_tensor_tensor(
         out=magnitude[:], in0=reduced[:], scalar=-1.0, in1=reduced[:], op0=ALU.mult, op1=ALU.max
     )
 
-    angle = const.tile([P, 2, BATCH, PAIRS, 2], F32)
+    angle = const.tile([P, 2, SLOTS, PAIRS, 2], F32)
     nc.vector.tensor_scalar(
         out=angle[:, 0],
-        in0=magnitude[:].unsqueeze(3).to_broadcast([P, BATCH, PAIRS, 2]),
+        in0=magnitude[:].unsqueeze(3).to_broadcast([P, SLOTS, PAIRS, 2]),
         scalar1=-1.0, scalar2=0.5 * math.pi, op0=ALU.mult, op1=ALU.add,
     )
-    nc.vector.tensor_copy(out=angle[:, 1, :, :, 0], in_=reduced[:])
-    nc.vector.tensor_scalar(out=angle[:, 1, :, :, 1], in0=reduced[:], scalar1=-1.0, scalar2=None, op0=ALU.mult)
+    nc.vector.tensor_copy(out=angle[:, 1, :, :, 1], in_=reduced[:])
+    nc.vector.tensor_scalar(out=angle[:, 1, :, :, 0], in0=reduced[:], scalar1=-1.0, scalar2=None, op0=ALU.mult)
     return angle
 
 
 def tile_ropeattention_pa_kernel(tc, x, coords, W_qkv, out_0, out_1, out_2):
     nc = tc.nc
     outputs = (out_0, out_1, out_2)
-    groups = [(which, c) for c in range(GROUPS_PER_OUTPUT) for which in (0, 2, 1)]
+    groups = [(0, 0), (2, 0), (1, 0), (0, 1), (2, 1), (1, 1), (0, 2), (2, 2), (1, 2)]
     last = len(groups) - 1
 
     with ExitStack() as ctx:
         const = ctx.enter_context(tc.tile_pool(name="const", bufs=1))
-        rows_pool = ctx.enter_context(tc.tile_pool(name="rows_pool", bufs=8))
-        spread_pool = ctx.enter_context(tc.tile_pool(name="spread_pool", bufs=4))
+        rows_pool = ctx.enter_context(tc.tile_pool(name="rows_pool", bufs=7))
+        spread_pool = ctx.enter_context(tc.tile_pool(name="spread_pool", bufs=6))
         stage = ctx.enter_context(tc.tile_pool(name="stage", bufs=2))
         packed = ctx.enter_context(tc.tile_pool(name="packed", bufs=4))
-        work = ctx.enter_context(tc.tile_pool(name="work", bufs=3))
-        results = ctx.enter_context(tc.tile_pool(name="results", bufs=1))
+        work = ctx.enter_context(tc.tile_pool(name="work", bufs=4))
+        results = ctx.enter_context(tc.tile_pool(name="results", bufs=2))
         flip_psum = ctx.enter_context(tc.psum_pool(name="flip_psum", bufs=4))
         acc_psum = ctx.enter_context(tc.psum_pool(name="acc_psum", bufs=4))
         ctx.enter_context(tc.manual_schedule())
 
-        coords_sb = const.tile([P, BATCH, 3], BF16)
-        nc.scalar.dma_start(out=coords_sb[:], in_=coords.rearrange("b s a -> s b a"))
+        def slot_rows(array, pair, b):
+            return array[PAIR_BATCHES * pair + b].rearrange("(m r) k -> m r k", r=RUN)
 
-        x_rows = []
-        for i in range(BATCH // 2):
-            x_pair = rows_pool.tile([P, 2, FEATURES], BF16, tag="rows")
-            x_rows.append(x_pair)
+        x_tiles = {}
 
-        def load_x(b):
-            nc.sync.dma_start(out=x_rows[b // 2][:, b % 2, :], in_=x[b])
+        def load_x(pair, r0, r1):
+            rows = rows_pool.tile([P, r1 - r0, FEATURES], BF16, tag="rows")
+            for b in range(PAIR_BATCHES):
+                nc.sync.dma_start(out=rows[b::PAIR_BATCHES], in_=slot_rows(x, pair, b)[:, r0:r1, :])
+            for r in range(r0, r1):
+                x_tiles[RUN * pair + r] = rows[:].bitcast(F32)[:, r - r0, :]
 
         w_rows = {}
 
-        def load_group(i, tiles_at_once):
+        def load_half(i, half, tiles_at_once):
             which, c = groups[i]
-            for half in range(2):
-                pair = rows_pool.tile([P, 2, FEATURES], BF16, tag="rows")
-                w_rows[(i, half)] = pair
-                for t in range(0, 2, tiles_at_once):
-                    row = which * OUT_COLS + c * GROUP_COLS + (2 * half + t) * P
-                    nc.sync.dma_start(
-                        out=pair[:, t : t + tiles_at_once, :],
-                        in_=W_qkv[row : row + tiles_at_once * P, :].rearrange("(t p) k -> p t k", p=P),
-                    )
+            rows = rows_pool.tile([P, 2, FEATURES], BF16, tag="rows")
+            w_rows[(i, half)] = rows
+            for t in range(0, 2, tiles_at_once):
+                first = which * OUT_COLS + c * GROUP_COLS + (2 * half + t) * P
+                nc.sync.dma_start(
+                    out=rows[:, t : t + tiles_at_once, :],
+                    in_=W_qkv[first : first + tiles_at_once * P, :].rearrange("(t p) k -> p t k", p=P),
+                )
 
-        load_x(0)
-        load_group(0, 1)
-        for b in range(1, BATCH):
-            load_x(b)
-        for i in range(1, last + 1):
-            load_group(i, 2)
+        coords_sb = const.tile([P, SLOTS // RUN, 16], BF16)
+        for pair in range(SLOTS // RUN):
+            for b in range(PAIR_BATCHES):
+                nc.scalar.dma_start(
+                    out=coords_sb[b::PAIR_BATCHES, pair, : RUN * 3], in_=slot_rows(coords, pair, b).rearrange("m r a -> m (r a)")
+                )
+        load_x(0, 0, 1)
+        load_half(0, 0, 1)
+        load_half(0, 1, 1)
+        load_x(0, 1, 2)
+        load_x(1, 0, 2)
+        to_load = [(i, half) for i in range(1, last + 1) for half in range(2)]
+        for n in range(6):
+            load_half(*to_load.pop(0), 2)
 
         freqs = frequencies(nc, const)
         warm = const.tile([P, 1], F32)
@@ -155,29 +166,28 @@ def tile_ropeattention_pa_kernel(tc, x, coords, W_qkv, out_0, out_1, out_2):
         identity = const.tile([P, P], F32)
         make_identity(nc, identity[:])
 
-        x_codes = const.tile([P, BATCH, PASSES, P], U32, align_bytes=64)
-        x_scales = const.tile([P, BATCH, PASSES, P], U8, align_bytes=64)
-        x_grouped = stage.tile([P, BATCH, PASSES, 4 * P], BF16, tag="grouped", align_bytes=64)
+        x_codes = const.tile([P, SLOTS, PASSES, P], U32, align_bytes=64)
+        x_scales = const.tile([P, SLOTS, PASSES, P], U8, align_bytes=64)
+        x_grouped = const.tile([P, SLOTS, PASSES, 4 * P], BF16, align_bytes=64)
 
         def every_second(words, g, u):
             return words[:, PASS_WORDS * g + u : PASS_WORDS * (g + 1) : 2]
 
-        def flip_x(b):
-            words = x_rows[b // 2][:].bitcast(F32)[:, b % 2, :]
-            for g0, g1 in ((0, 2), (2, 3)):
+        def flip_x(s, copies):
+            for (g0, g1), copy in zip(((0, 2), (2, 3)), copies):
                 flipped = flip_psum.tile([P, g1 - g0, 2, P], F32, tag="flipped")
                 for g in range(g0, g1):
                     for u in range(2):
-                        nc.tensor.transpose(flipped[:, g - g0, u, :], every_second(words, g, u), identity[:])
-                nc.scalar.copy(
-                    out=x_grouped[:, b, g0:g1, :].bitcast(F32).rearrange("q g (c u) -> q g c u", u=2),
+                        nc.tensor.transpose(flipped[:, g - g0, u, :], every_second(x_tiles[s], g, u), identity[:])
+                copy(
+                    out=x_grouped[:, s, g0:g1, :].bitcast(F32).rearrange("q g (c u) -> q g c u", u=2),
                     in_=flipped[:].rearrange("q g u c -> q g c u"),
                 )
 
         def quantise_x(first, widths):
-            codes = x_codes[:].rearrange("q b g c -> q (b g c)")
-            scales = x_scales[:].rearrange("q b g c -> q (b g c)")
-            grouped = x_grouped[:].rearrange("q b g w -> q (b g w)")
+            codes = x_codes[:].rearrange("q s g c -> q (s g c)")
+            scales = x_scales[:].rearrange("q s g c -> q (s g c)")
+            grouped = x_grouped[:].rearrange("q s g w -> q (s g w)")
             for n in widths:
                 lo, hi = P * first, P * (first + n)
                 nc.vector.quantize_mx(
@@ -188,42 +198,40 @@ def tile_ropeattention_pa_kernel(tc, x, coords, W_qkv, out_0, out_1, out_2):
         spread = {}
 
         def spread_tile(copy, i, t):
-            tile = spread_pool.tile([P, PASSES, 2, P], F32, tag="spread")
+            tile = spread_pool.tile([P, 2, PASSES, P], F32, tag="spread")
             words = w_rows[(i, t // 2)][:].bitcast(F32)[:, t % 2, :]
-            copy(out=tile[:], in_=words.rearrange("r (g q u) -> r g u q", g=PASSES, u=2))
+            copy(out=tile[:], in_=words.rearrange("r (g q u) -> r u g q", g=PASSES, u=2))
             spread[(i, t)] = tile
 
-        def flip_bank(i, g, half):
-            flipped = flip_psum.tile([P, 2, 2 * P], F32, tag="flipped")
-            for u in range(2):
-                for t in range(2):
-                    if (i, 2 * half + t) in spread:
-                        words = spread[(i, 2 * half + t)][:, g, u, :]
-                    else:
-                        words = every_second(w_rows[(i, half)][:].bitcast(F32)[:, t, :], g, u)
-                    nc.tensor.transpose(flipped[:, u, P * t : P * t + P], words, identity[:])
-            return flipped
+        def tile_words(i, t, g, u):
+            if (i, t) in spread:
+                return spread[(i, t)][:, u, g, :]
+            return every_second(w_rows[(i, t // 2)][:].bitcast(F32)[:, t % 2, :], g, u)
 
         operands = {}
 
-        def prepare(i, banks, on_vector, parts):
+        def prepare(i, banks, copies):
             if i not in operands:
                 w_codes = packed.tile([P, PASSES, GROUP_COLS], U32, tag="w_codes", align_bytes=64)
                 w_scales = packed.tile([P, PASSES, GROUP_COLS], U8, tag="w_scales", align_bytes=64)
                 grouped = stage.tile([P, PASSES, 4 * GROUP_COLS], BF16, tag="grouped", align_bytes=64)
                 operands[i] = (w_codes, w_scales, grouped)
-            w_codes, w_scales, grouped = operands[i]
-            for n, (g, half) in enumerate(banks):
-                copy = nc.vector.tensor_copy if n >= len(banks) - on_vector else nc.scalar.copy
-                flipped = flip_bank(i, g, half)
+            grouped = operands[i][2]
+            for (g, half), copy in zip(banks, copies):
+                flipped = flip_psum.tile([P, 2, 2 * P], F32, tag="flipped")
+                for t in range(2):
+                    for u in range(2):
+                        nc.tensor.transpose(flipped[:, u, P * t : P * t + P], tile_words(i, 2 * half + t, g, u), identity[:])
                 words = grouped[:, g, :].bitcast(F32)[:, 512 * half : 512 * half + 512]
                 copy(out=words.rearrange("q (c u) -> q c u", u=2), in_=flipped[:].rearrange("q u c -> q c u"))
-            for g0, g1 in parts:
-                nc.vector.quantize_mx(
-                    out=w_codes[:, g0:g1, :].rearrange("q g c -> q (g c)").bitcast(FP8X4),
-                    scales=w_scales[:, g0:g1, :].rearrange("q g c -> q (g c)"),
-                    in_=grouped[:, g0:g1, :].rearrange("q g w -> q (g w)"),
-                )
+
+        def quantise(i, g0, g1):
+            w_codes, w_scales, grouped = operands[i]
+            nc.vector.quantize_mx(
+                out=w_codes[:, g0:g1, :].rearrange("q g c -> q (g c)").bitcast(FP8X4),
+                scales=w_scales[:, g0:g1, :].rearrange("q g c -> q (g c)"),
+                in_=grouped[:, g0:g1, :].rearrange("q g w -> q (g w)"),
+            )
 
         def quantise_half(i, half):
             w_codes, w_scales, grouped = operands[i]
@@ -235,14 +243,14 @@ def tile_ropeattention_pa_kernel(tc, x, coords, W_qkv, out_0, out_1, out_2):
                     in_=grouped[:, g, 4 * lo : 4 * hi],
                 )
 
-        def multiply(i, b):
+        def multiply(i, s):
             w_codes, w_scales, grouped = operands[i]
             acc = acc_psum.tile([P, GROUP_COLS], F32, tag="acc")
             for g in range(PASSES):
                 nc.tensor.matmul_mx(
                     out=acc[:],
-                    lhsT=x_codes[:, b, g, :].bitcast(FP8X4),
-                    lhsT_scale=x_scales[:, b, g, :],
+                    lhsT=x_codes[:, s, g, :].bitcast(FP8X4),
+                    lhsT_scale=x_scales[:, s, g, :],
                     rhs=w_codes[:, g, :].bitcast(FP8X4),
                     rhs_scale=w_scales[:, g, :],
                     start=(g == 0),
@@ -250,116 +258,161 @@ def tile_ropeattention_pa_kernel(tc, x, coords, W_qkv, out_0, out_1, out_2):
                 )
             return acc
 
+        def pieces(c):
+            cuts = []
+            column = 0
+            while column < GROUP_COLS:
+                head, feature = divmod(GROUP_COLS * c + column, HEAD_DIM)
+                whole = (GROUP_COLS - column) // HEAD_DIM * HEAD_DIM
+                if feature == 0 and whole > 0:
+                    n = whole
+                else:
+                    n = min(HEAD_DIM - feature, GROUP_COLS - column)
+                cuts.append((column, n, head, feature))
+                column += n
+            return cuts
+
+        def heads_of(c):
+            return GROUP_COLS * c // HEAD_DIM, GROUP_COLS * (c + 1) // HEAD_DIM
+
         result_tiles = {}
 
-        def columns_of(i, b):
-            which, c = groups[i]
-            if c == 0:
-                result_row = results.tile([P, OUT_COLS], F32, tag="result_%d_%d" % (which, b))
-                result_tiles[(which, b)] = result_row
-            return result_tiles[(which, b)][:, GROUP_COLS * c : GROUP_COLS * (c + 1)]
+        def result_of(which, pair, head):
+            c = 0
+            while head >= heads_of(c)[1]:
+                c += 1
+            if (which, pair, c) not in result_tiles:
+                result = results.tile([P, TABLE_HEADS, RUN, HEAD_DIM], F32, tag="result_%d_%d" % (which, pair))
+                result_tiles[(which, pair, c)] = result
+            return result_tiles[(which, pair, c)], head - heads_of(c)[0]
 
-        def times_table(i, b, acc):
-            which, c = groups[i]
-            products = work.tile([P, 2, GROUP_COLS], F32, tag="products")
+        def result_piece(which, s, n, head, feature):
+            result, place = result_of(which, s // RUN, head)
+            if n < HEAD_DIM:
+                return result[:, place, s % RUN, feature : feature + n]
+            return result[:, place : place + n // HEAD_DIM, s % RUN, :]
+
+        def by_head(columns, n):
+            return columns if n < HEAD_DIM else columns.rearrange("p (h d) -> p h d", d=HEAD_DIM)
+
+        def table_of(c, s, plane):
             phase = c * GROUP_COLS % HEAD_DIM
-            nc.vector.tensor_tensor(
-                out=products[:],
-                in0=acc[:].unsqueeze(1).to_broadcast([P, 2, GROUP_COLS]),
-                in1=rot[:, :, b, phase : phase + GROUP_COLS],
-                op=ALU.mult,
-            )
+            return rot[:, plane, s, phase : phase + GROUP_COLS]
+
+        def times_cos(i, s, acc):
+            products = work.tile([P, 2, GROUP_COLS], F32, tag="products")
+            nc.vector.tensor_tensor(out=products[:, 0, :], in0=acc[:], in1=table_of(groups[i][1], s, 0), op=ALU.mult)
             return products
 
-        def add_planes(engine, i, b, products):
-            pairs = "s (n w) -> s n w"
-            engine.tensor_tensor(
-                out=columns_of(i, b).rearrange(pairs, w=2),
-                in0=products[:, 0, :].rearrange(pairs, w=2),
-                in1=products[:, 1, :].rearrange(pairs, w=2)[:, :, ::-1],
-                op=ALU.add,
+        def times_sin(i, s, acc, products):
+            in_pairs = "p (n w) -> p n w"
+            nc.vector.tensor_tensor(
+                out=products[:, 1, :].rearrange(in_pairs, w=2),
+                in0=acc[:].rearrange(in_pairs, w=2)[:, :, ::-1],
+                in1=table_of(groups[i][1], s, 1).rearrange(in_pairs, w=2),
+                op=ALU.mult,
             )
 
-        def store(i, b):
+        def add_planes(i, s, products, engine=nc.gpsimd):
             which, c = groups[i]
-            h0 = GROUP_COLS * c // HEAD_DIM
-            h1 = GROUP_COLS * (c + 1) // HEAD_DIM
-            nc.sync.dma_start(
-                out=outputs[which][b, h0:h1].rearrange("h s d -> s h d"),
-                in_=result_tiles[(which, b)][:, HEAD_DIM * h0 : HEAD_DIM * h1].rearrange("s (h d) -> s h d", d=HEAD_DIM),
-            )
+            for column, n, head, feature in pieces(c):
+                engine.tensor_tensor(
+                    out=result_piece(which, s, n, head, feature),
+                    in0=by_head(products[:, 0, column : column + n], n),
+                    in1=by_head(products[:, 1, column : column + n], n),
+                    op=ALU.add,
+                )
 
-        rot = const.tile([P, 2, BATCH, TABLE_HEADS * HEAD_DIM], F32)
+        def copy_plain(copy, i, s, acc):
+            which, c = groups[i]
+            for column, n, head, feature in pieces(c):
+                copy(out=result_piece(which, s, n, head, feature), in_=by_head(acc[:, column : column + n], n))
+
+        def store(which, c, pair):
+            h0, h1 = heads_of(c)
+            result = result_of(which, pair, h0)[0]
+            for b in range(PAIR_BATCHES):
+                nc.sync.dma_start(
+                    out=outputs[which][PAIR_BATCHES * pair + b, h0:h1].rearrange("h (m r) d -> m h (r d)", r=RUN),
+                    in_=result[b::PAIR_BATCHES, 0 : h1 - h0].rearrange("p h r d -> p h (r d)"),
+                )
+
+        rot = const.tile([P, 2, SLOTS, TABLE_HEADS * HEAD_DIM], F32)
 
         def fill_table():
             nc.scalar.activation(
-                out=rot[:, :, :, :HEAD_DIM],
-                in_=angle[:].rearrange("s i b n e -> s i b (n e)"),
-                func=ACT.Sin,
+                out=rot[:, :, :, :HEAD_DIM], in_=angle[:].rearrange("p i s n e -> p i s (n e)"), func=ACT.Sin
             )
 
-        def repeat_table(b):
-            shape = [P, 2, TABLE_HEADS - 1, HEAD_DIM]
+        def repeat_table(s):
             nc.vector.tensor_copy(
-                out=rot[:, :, b, HEAD_DIM:].rearrange("s i (h d) -> s i h d", d=HEAD_DIM),
-                in_=rot[:, :, b, :HEAD_DIM].unsqueeze(2).to_broadcast(shape),
+                out=rot[:, :, s, HEAD_DIM:].rearrange("p i (h d) -> p i h d", d=HEAD_DIM),
+                in_=rot[:, :, s, :HEAD_DIM].unsqueeze(2).to_broadcast([P, 2, TABLE_HEADS - 1, HEAD_DIM]),
             )
 
+        by_scalar, by_vector = nc.scalar.copy, nc.vector.tensor_copy
         by_pass = [(g, half) for g in range(PASSES) for half in range(2)]
-        by_arrival = [(g, half) for half in range(2) for g in range(PASSES)]
 
-        reduced = rotation_arguments(nc, const, coords_sb, freqs)
-        flip_x(0)
-        quantise_x(0, (2, 1))
-        prepare(0, by_arrival[:3], 0, ())
-        quantise_half(0, 0)
-        prepare(0, by_arrival[3:], 0, ())
-        quantise_half(0, 1)
-        angle = rotation_angles(nc, const, reduced)
-        flip_x(1)
-        fill_table()
-        repeat_table(0)
-        rotated = [(3 * c + w, b) for c in range(GROUPS_PER_OUTPUT) for w in (0, 2) for b in range(BATCH)]
-        plain = [(3 * c + 1, b) for c in range(GROUPS_PER_OUTPUT) for b in range(BATCH)]
+        def finish(i, s):
+            if s % RUN == RUN - 1:
+                store(*groups[i], s // RUN)
+
+        rotated = [(i, s) for i in range(last + 1) if groups[i][0] != 2 for s in range(SLOTS)]
+        plain = [(i, s) for i in range(last + 1) if groups[i][0] == 2 for s in range(SLOTS)]
         units = []
         while rotated or plain:
             turn = plain if plain and (len(units) % 3 == 0 and len(units) >= 3 or not rotated) else rotated
             units.append(turn.pop(0))
-        slot_units = [units[:1], units[1:4]] + [units[n : n + 2] for n in range(4, len(units), 2)]
-        first_slot = {}
-        for n, slot in enumerate(slot_units):
-            for i, b in slot:
-                first_slot.setdefault(i, n)
-        prep_slot = {last: first_slot[last] - 1}
+        steps = [units[:1], units[1:4]] + [units[n : n + 2] for n in range(4, len(units), 2)]
+        first_step = {}
+        for n, step in enumerate(steps):
+            for i, s in step:
+                first_step.setdefault(i, n)
+        prep_step = {last: first_step[last] - 1}
         for j in range(last - 1, 0, -1):
-            prep_slot[j] = max(1, min(first_slot[j] - 1, prep_slot[j + 1] - 1))
-        slots = [([j for j in range(1, last + 1) if prep_slot[j] == n], slot) for n, slot in enumerate(slot_units)]
-        plan = {j: [(1, nc.scalar.copy, 2, True)] for j in range(3, last + 1)}
-        for n, (prep, units) in enumerate(slots):
+            prep_step[j] = max(1, min(first_step[j] - 1, prep_step[j + 1] - 1))
+
+        reduced = rotation_arguments(nc, const, coords_sb, freqs)
+        flip_x(0, (by_scalar, by_scalar))
+        quantise_x(0, (2, 1))
+        for half in range(2):
+            prepare(0, [(g, half) for g in range(PASSES)], ((by_scalar,) * 3, (by_scalar,) * 3)[half])
+            quantise_half(0, half)
+        angle = rotation_angles(nc, const, reduced)
+        flip_x(1, (by_scalar, by_scalar))
+        fill_table()
+        repeat_table(0)
+
+        plan = {j: [(1, 2)] for j in range(3, last + 1)}
+        for n, step in enumerate(steps):
             if n == 1:
-                for b in range(2, BATCH):
-                    flip_x(b)
+                for s in (2, 3):
+                    flip_x(s, (by_scalar, by_scalar))
                 quantise_x(3, (8, 1))
-                for b in range(1, BATCH):
-                    repeat_table(b)
+                for s in range(1, SLOTS):
+                    repeat_table(s)
             for j in plan:
-                for t, copy, ahead, before in plan[j]:
-                    if before and prep_slot[j] == n + ahead:
-                        spread_tile(copy, j, t)
-            for j in prep:
-                prepare(j, by_pass, 0, ((0, 2), (2, 3)))
-            accs = [multiply(i, b) for i, b in units]
+                for t, ahead in plan[j]:
+                    if prep_step[j] == n + ahead:
+                        spread_tile(by_scalar, j, t)
+
+            for j in range(1, last + 1):
+                if prep_step[j] == n:
+                    prepare(j, by_pass, (by_scalar,) * 6)
+                    for g0, g1 in ((0, 2), (2, 3)):
+                        quantise(j, g0, g1)
+                    for k in range(2):
+                        if to_load:
+                            load_half(*to_load.pop(0), 2)
+            accs = [multiply(i, s) for i, s in step]
             products = {}
-            for k, (i, b) in enumerate(units):
+            for k, (i, s) in enumerate(step):
                 if groups[i][0] == 2:
-                    nc.scalar.copy(out=columns_of(i, b), in_=accs[k][:])
+                    copy_plain(by_scalar, i, s, accs[k])
                 else:
-                    products[(i, b)] = times_table(i, b, accs[k])
-            for k, (i, b) in enumerate(units):
+                    products[k] = times_cos(i, s, accs[k])
+                    times_sin(i, s, accs[k], products[k])
+            for k, (i, s) in enumerate(step):
                 if groups[i][0] != 2:
-                    add_planes(nc.vector if False else nc.gpsimd, i, b, products[(i, b)])
-                store(i, b)
-            for j in plan:
-                for t, copy, ahead, before in plan[j]:
-                    if not before and prep_slot[j] == n + ahead:
-                        spread_tile(copy, j, t)
+                    add_planes(i, s, products[k])
+                finish(i, s)

@@ -103,7 +103,7 @@ def rotation_angles(nc, const, reduced):
 def tile_ropeattention_pa_kernel(tc, x, coords, W_qkv, out_0, out_1, out_2):
     nc = tc.nc
     outputs = (out_0, out_1, out_2)
-    groups = [(0, 0), (2, 0), (1, 0), (0, 1), (2, 1), (1, 1), (0, 2), (2, 2), (1, 2)]
+    groups = [(0, 0), (2, 0), (1, 0), (0, 1), (2, 1), (1, 1), (0, 2), (1, 2), (2, 2)]
     last = len(groups) - 1
 
     with ExitStack() as ctx:
@@ -359,60 +359,69 @@ def tile_ropeattention_pa_kernel(tc, x, coords, W_qkv, out_0, out_1, out_2):
 
         rotated = [(i, s) for i in range(last + 1) if groups[i][0] != 2 for s in range(SLOTS)]
         plain = [(i, s) for i in range(last + 1) if groups[i][0] == 2 for s in range(SLOTS)]
-        units = []
+        steps = []
         while rotated or plain:
-            turn = plain if plain and (len(units) % 3 == 0 and len(units) >= 3 or not rotated) else rotated
-            units.append(turn.pop(0))
-        steps = [units[:1], units[1:4]] + [units[n : n + 2] for n in range(4, len(units), 2)]
-        first_step = {}
-        for n, step in enumerate(steps):
-            for i, s in step:
-                first_step.setdefault(i, n)
-        prep_step = {last: first_step[last] - 1}
-        for j in range(last - 1, 0, -1):
-            prep_step[j] = max(1, min(first_step[j] - 1, prep_step[j + 1] - 1))
+            n = len(steps)
+            units = []
+            for kind in ((rotated, rotated) if n % 3 == 1 or n < 2 else (plain, rotated)) if rotated else (plain, plain):
+                if kind and 2 * kind[0][0] <= n:
+                    units.append(kind.pop(0))
+            steps.append(units)
 
         reduced = rotation_arguments(nc, const, coords_sb, freqs)
         flip_x(0, (by_scalar, by_scalar))
         quantise_x(0, (2, 1))
         for half in range(2):
-            prepare(0, [(g, half) for g in range(PASSES)], ((by_scalar,) * 3, (by_scalar,) * 3)[half])
+            prepare(0, [(g, half) for g in range(PASSES)], ((by_scalar, by_scalar, by_vector), (by_scalar, by_scalar, by_vector))[half])
             quantise_half(0, half)
-        angle = rotation_angles(nc, const, reduced)
         flip_x(1, (by_scalar, by_scalar))
+        angle = rotation_angles(nc, const, reduced)
+        quantise_x(3, (2, 1))
+        for s in (2, 3):
+            flip_x(s, (by_scalar, by_scalar))
+        quantise_x(6, (4, 2))
         fill_table()
         repeat_table(0)
+        repeat_table(1)
 
-        plan = {j: [(1, 2)] for j in range(3, last + 1)}
-        for n, step in enumerate(steps):
-            if n == 1:
-                for s in (2, 3):
-                    flip_x(s, (by_scalar, by_scalar))
-                quantise_x(3, (8, 1))
-                for s in range(1, SLOTS):
-                    repeat_table(s)
-            for j in plan:
-                for t, ahead in plan[j]:
-                    if prep_step[j] == n + ahead:
-                        spread_tile(by_scalar, j, t)
-
-            for j in range(1, last + 1):
-                if prep_step[j] == n:
-                    prepare(j, by_pass, (by_scalar,) * 6)
-                    for g0, g1 in ((0, 2), (2, 3)):
-                        quantise(j, g0, g1)
+        late = []
+        for n, units in enumerate(steps):
+            j, part = n // 2 + 1, n % 2
+            if j == 1:
+                prepare(j, [(g, part) for g in range(PASSES)], (by_scalar, by_scalar, by_scalar))
+            elif j <= last:
+                prepare(j, by_pass[3 * part : 3 * part + 3], (by_scalar, by_scalar, by_scalar))
+            accs = [multiply(i, s) for i, s in units]
+            if j <= last:
+                if j == 1:
+                    quantise_half(j, part)
+                else:
+                    quantise(j, *((0, 1), (1, 3))[part])
+                if part == 1:
                     for k in range(2):
                         if to_load:
                             load_half(*to_load.pop(0), 2)
-            accs = [multiply(i, s) for i, s in step]
-            products = {}
-            for k, (i, s) in enumerate(step):
-                if groups[i][0] == 2:
-                    copy_plain(by_scalar, i, s, accs[k])
-                else:
-                    products[k] = times_cos(i, s, accs[k])
-                    times_sin(i, s, accs[k], products[k])
-            for k, (i, s) in enumerate(step):
-                if groups[i][0] != 2:
-                    add_planes(i, s, products[k])
+                if n >= 1 and n % 2 == 0:
+                    jj = (n + 3) // 2 + 1
+                    if jj <= last:
+                        spread_tile(by_scalar, jj, 1)
+            if n == 0:
+                for s in (2, 3):
+                    repeat_table(s)
+            for i, s, acc, products in late:
+                times_sin(i, s, acc, products)
+                add_planes(i, s, products)
                 finish(i, s)
+            late = []
+            for k, (i, s) in enumerate(units):
+                if groups[i][0] == 2:
+                    copy_plain(by_vector if n > 15 and k % 2 else by_scalar, i, s, accs[k])
+                    finish(i, s)
+                else:
+                    products = times_cos(i, s, accs[k])
+                    if False:
+                        late.append((i, s, accs[k], products))
+                    else:
+                        times_sin(i, s, accs[k], products)
+                        add_planes(i, s, products, nc.vector if False else nc.gpsimd)
+                        finish(i, s)

@@ -28,9 +28,11 @@ PASSES = FEATURES // K_PASS
 PASS_WORDS = K_PASS // 2
 OUT_COLS = HEADS * HEAD_DIM
 
-GROUP_COLS = 512
-CHUNKS = OUT_COLS // GROUP_COLS
-TABLE_HEADS = 6
+GROUP_HEADS = 4
+GROUP_COLS = GROUP_HEADS * HEAD_DIM
+TILES = GROUP_COLS // P
+QUARTERS = HEADS // GROUP_HEADS
+PARTS = ((0, 2 * P), (2 * P, GROUP_COLS))
 
 FLOPS = 2 * BATCH * P * FEATURES * 3 * OUT_COLS
 
@@ -103,17 +105,17 @@ def rotation_angles(nc, const, reduced):
 def tile_ropeattention_pa_kernel(tc, x, coords, W_qkv, out_0, out_1, out_2):
     nc = tc.nc
     outputs = (out_0, out_1, out_2)
-    groups = [(0, 0), (2, 0), (1, 0), (0, 1), (2, 1), (1, 1), (0, 2), (1, 2), (2, 2)]
+    groups = [(which, c) for c in range(QUARTERS) for which in ((0, 2, 1) if c < QUARTERS - 1 else (0, 1, 2))]
     last = len(groups) - 1
 
     with ExitStack() as ctx:
         const = ctx.enter_context(tc.tile_pool(name="const", bufs=1))
-        rows_pool = ctx.enter_context(tc.tile_pool(name="rows_pool", bufs=7))
-        spread_pool = ctx.enter_context(tc.tile_pool(name="spread_pool", bufs=6))
+        rows_pool = ctx.enter_context(tc.tile_pool(name="rows_pool", bufs=5))
+        spread_pool = ctx.enter_context(tc.tile_pool(name="spread_pool", bufs=3))
         stage = ctx.enter_context(tc.tile_pool(name="stage", bufs=2))
         packed = ctx.enter_context(tc.tile_pool(name="packed", bufs=4))
-        work = ctx.enter_context(tc.tile_pool(name="work", bufs=4))
-        results = ctx.enter_context(tc.tile_pool(name="results", bufs=2))
+        work = ctx.enter_context(tc.tile_pool(name="work", bufs=6))
+        results = ctx.enter_context(tc.tile_pool(name="results", bufs=12))
         flip_psum = ctx.enter_context(tc.psum_pool(name="flip_psum", bufs=4))
         acc_psum = ctx.enter_context(tc.psum_pool(name="acc_psum", bufs=4))
         ctx.enter_context(tc.manual_schedule())
@@ -124,7 +126,7 @@ def tile_ropeattention_pa_kernel(tc, x, coords, W_qkv, out_0, out_1, out_2):
         x_tiles = {}
 
         def load_x(pair, r0, r1):
-            rows = rows_pool.tile([P, r1 - r0, FEATURES], BF16, tag="rows")
+            rows = const.tile([P, r1 - r0, FEATURES], BF16, name="x_%d_%d" % (pair, r0))
             for b in range(PAIR_BATCHES):
                 nc.sync.dma_start(out=rows[b::PAIR_BATCHES], in_=slot_rows(x, pair, b)[:, r0:r1, :])
             for r in range(r0, r1):
@@ -132,15 +134,15 @@ def tile_ropeattention_pa_kernel(tc, x, coords, W_qkv, out_0, out_1, out_2):
 
         w_rows = {}
 
-        def load_half(i, half, tiles_at_once):
+        def load_group(i, cuts):
             which, c = groups[i]
-            rows = rows_pool.tile([P, 2, FEATURES], BF16, tag="rows")
-            w_rows[(i, half)] = rows
-            for t in range(0, 2, tiles_at_once):
-                first = which * OUT_COLS + c * GROUP_COLS + (2 * half + t) * P
+            rows = rows_pool.tile([P, TILES, FEATURES], BF16, tag="rows")
+            w_rows[i] = rows
+            first = which * OUT_COLS + c * GROUP_COLS
+            for t0, t1 in cuts:
                 nc.sync.dma_start(
-                    out=rows[:, t : t + tiles_at_once, :],
-                    in_=W_qkv[first : first + tiles_at_once * P, :].rearrange("(t p) k -> p t k", p=P),
+                    out=rows[:, t0:t1, :],
+                    in_=W_qkv[first + t0 * P : first + t1 * P, :].rearrange("(t p) k -> p t k", p=P),
                 )
 
         coords_sb = const.tile([P, SLOTS // RUN, 16], BF16)
@@ -150,13 +152,12 @@ def tile_ropeattention_pa_kernel(tc, x, coords, W_qkv, out_0, out_1, out_2):
                     out=coords_sb[b::PAIR_BATCHES, pair, : RUN * 3], in_=slot_rows(coords, pair, b).rearrange("m r a -> m (r a)")
                 )
         load_x(0, 0, 1)
-        load_half(0, 0, 1)
-        load_half(0, 1, 1)
+        load_group(0, [(t, t + 1) for t in range(TILES)])
         load_x(0, 1, 2)
         load_x(1, 0, 2)
-        to_load = [(i, half) for i in range(1, last + 1) for half in range(2)]
-        for n in range(6):
-            load_half(*to_load.pop(0), 2)
+        whole = [(0, TILES)]
+        for i in range(1, 6):
+            load_group(i, whole)
 
         freqs = frequencies(nc, const)
         warm = const.tile([P, 1], F32)
@@ -199,16 +200,19 @@ def tile_ropeattention_pa_kernel(tc, x, coords, W_qkv, out_0, out_1, out_2):
 
         def spread_tile(copy, i, t):
             tile = spread_pool.tile([P, 2, PASSES, P], F32, tag="spread")
-            words = w_rows[(i, t // 2)][:].bitcast(F32)[:, t % 2, :]
+            words = w_rows[i][:].bitcast(F32)[:, t, :]
             copy(out=tile[:], in_=words.rearrange("r (g q u) -> r u g q", g=PASSES, u=2))
             spread[(i, t)] = tile
 
         def tile_words(i, t, g, u):
             if (i, t) in spread:
                 return spread[(i, t)][:, u, g, :]
-            return every_second(w_rows[(i, t // 2)][:].bitcast(F32)[:, t % 2, :], g, u)
+            return every_second(w_rows[i][:].bitcast(F32)[:, t, :], g, u)
 
         operands = {}
+
+        WIDE = [(g, g + 1, 0, 2) for g in range(PASSES)]
+        NARROW = [(0, 2, 2, 3), (2, 3, 2, 3)]
 
         def prepare(i, banks, copies):
             if i not in operands:
@@ -217,91 +221,56 @@ def tile_ropeattention_pa_kernel(tc, x, coords, W_qkv, out_0, out_1, out_2):
                 grouped = stage.tile([P, PASSES, 4 * GROUP_COLS], BF16, tag="grouped", align_bytes=64)
                 operands[i] = (w_codes, w_scales, grouped)
             grouped = operands[i][2]
-            for (g, half), copy in zip(banks, copies):
-                flipped = flip_psum.tile([P, 2, 2 * P], F32, tag="flipped")
-                for t in range(2):
-                    for u in range(2):
-                        nc.tensor.transpose(flipped[:, u, P * t : P * t + P], tile_words(i, 2 * half + t, g, u), identity[:])
-                words = grouped[:, g, :].bitcast(F32)[:, 512 * half : 512 * half + 512]
-                copy(out=words.rearrange("q (c u) -> q c u", u=2), in_=flipped[:].rearrange("q u c -> q c u"))
+            for (g0, g1, t0, t1), copy in zip(banks, copies):
+                flipped = flip_psum.tile([P, g1 - g0, 2, P * (t1 - t0)], F32, tag="flipped")
+                for t in range(t0, t1):
+                    for g in range(g0, g1):
+                        for u in range(2):
+                            nc.tensor.transpose(
+                                flipped[:, g - g0, u, P * (t - t0) : P * (t - t0 + 1)], tile_words(i, t, g, u), identity[:]
+                            )
+                words = grouped[:, g0:g1, :].bitcast(F32)[:, :, 2 * P * t0 : 2 * P * t1]
+                copy(out=words.rearrange("q g (c u) -> q g c u", u=2), in_=flipped[:].rearrange("q g u c -> q g c u"))
 
-        def quantise(i, g0, g1):
+        def quantise(i, widths):
             w_codes, w_scales, grouped = operands[i]
-            nc.vector.quantize_mx(
-                out=w_codes[:, g0:g1, :].rearrange("q g c -> q (g c)").bitcast(FP8X4),
-                scales=w_scales[:, g0:g1, :].rearrange("q g c -> q (g c)"),
-                in_=grouped[:, g0:g1, :].rearrange("q g w -> q (g w)"),
-            )
-
-        def quantise_half(i, half):
-            w_codes, w_scales, grouped = operands[i]
-            lo, hi = 256 * half, 256 * half + 256
-            for g in range(PASSES):
+            codes = w_codes[:].rearrange("q g c -> q (g c)")
+            scales = w_scales[:].rearrange("q g c -> q (g c)")
+            values = grouped[:].rearrange("q g w -> q (g w)")
+            lo = 0
+            for n in widths:
                 nc.vector.quantize_mx(
-                    out=w_codes[:, g, lo:hi].bitcast(FP8X4),
-                    scales=w_scales[:, g, lo:hi],
-                    in_=grouped[:, g, 4 * lo : 4 * hi],
+                    out=codes[:, lo : lo + n].bitcast(FP8X4), scales=scales[:, lo : lo + n], in_=values[:, 4 * lo : 4 * (lo + n)]
                 )
+                lo += n
 
         def multiply(i, s):
             w_codes, w_scales, grouped = operands[i]
             acc = acc_psum.tile([P, GROUP_COLS], F32, tag="acc")
-            for g in range(PASSES):
-                nc.tensor.matmul_mx(
-                    out=acc[:],
-                    lhsT=x_codes[:, s, g, :].bitcast(FP8X4),
-                    lhsT_scale=x_scales[:, s, g, :],
-                    rhs=w_codes[:, g, :].bitcast(FP8X4),
-                    rhs_scale=w_scales[:, g, :],
-                    start=(g == 0),
-                    stop=(g == PASSES - 1),
-                )
+            for lo, hi in PARTS:
+                for g in range(PASSES):
+                    nc.tensor.matmul_mx(
+                        out=acc[:, lo:hi],
+                        lhsT=x_codes[:, s, g, :].bitcast(FP8X4),
+                        lhsT_scale=x_scales[:, s, g, :],
+                        rhs=w_codes[:, g, lo:hi].bitcast(FP8X4),
+                        rhs_scale=w_scales[:, g, lo:hi],
+                        start=(g == 0),
+                        stop=(g == PASSES - 1),
+                    )
             return acc
-
-        def pieces(c):
-            cuts = []
-            column = 0
-            while column < GROUP_COLS:
-                head, feature = divmod(GROUP_COLS * c + column, HEAD_DIM)
-                whole = (GROUP_COLS - column) // HEAD_DIM * HEAD_DIM
-                if feature == 0 and whole > 0:
-                    n = whole
-                else:
-                    n = min(HEAD_DIM - feature, GROUP_COLS - column)
-                cuts.append((column, n, head, feature))
-                column += n
-            return cuts
-
-        def heads_of(c):
-            return GROUP_COLS * c // HEAD_DIM, GROUP_COLS * (c + 1) // HEAD_DIM
 
         result_tiles = {}
 
-        def result_of(which, pair, head):
-            c = 0
-            while head >= heads_of(c)[1]:
-                c += 1
-            if (which, pair, c) not in result_tiles:
-                result = results.tile([P, TABLE_HEADS, RUN, HEAD_DIM], F32, tag="result_%d_%d" % (which, pair))
-                result_tiles[(which, pair, c)] = result
-            return result_tiles[(which, pair, c)], head - heads_of(c)[0]
-
-        def result_piece(which, s, n, head, feature):
-            result, place = result_of(which, s // RUN, head)
-            if n < HEAD_DIM:
-                return result[:, place, s % RUN, feature : feature + n]
-            return result[:, place : place + n // HEAD_DIM, s % RUN, :]
-
-        def by_head(columns, n):
-            return columns if n < HEAD_DIM else columns.rearrange("p (h d) -> p h d", d=HEAD_DIM)
-
-        def table_of(c, s, plane):
-            phase = c * GROUP_COLS % HEAD_DIM
-            return rot[:, plane, s, phase : phase + GROUP_COLS]
+        def result_of(i, s):
+            if (i, s // RUN) not in result_tiles:
+                result = results.tile([P, GROUP_HEADS, RUN, HEAD_DIM], F32, tag="result")
+                result_tiles[(i, s // RUN)] = result
+            return result_tiles[(i, s // RUN)][:, :, s % RUN, :]
 
         def times_cos(i, s, acc):
             products = work.tile([P, 2, GROUP_COLS], F32, tag="products")
-            nc.vector.tensor_tensor(out=products[:, 0, :], in0=acc[:], in1=table_of(groups[i][1], s, 0), op=ALU.mult)
+            nc.vector.tensor_tensor(out=products[:, 0, :], in0=acc[:], in1=rot[:, 0, s, :], op=ALU.mult)
             return products
 
         def times_sin(i, s, acc, products):
@@ -309,35 +278,35 @@ def tile_ropeattention_pa_kernel(tc, x, coords, W_qkv, out_0, out_1, out_2):
             nc.vector.tensor_tensor(
                 out=products[:, 1, :].rearrange(in_pairs, w=2),
                 in0=acc[:].rearrange(in_pairs, w=2)[:, :, ::-1],
-                in1=table_of(groups[i][1], s, 1).rearrange(in_pairs, w=2),
+                in1=rot[:, 1, s, :].rearrange(in_pairs, w=2),
                 op=ALU.mult,
             )
 
-        def add_planes(i, s, products, engine=nc.gpsimd):
-            which, c = groups[i]
-            for column, n, head, feature in pieces(c):
-                engine.tensor_tensor(
-                    out=result_piece(which, s, n, head, feature),
-                    in0=by_head(products[:, 0, column : column + n], n),
-                    in1=by_head(products[:, 1, column : column + n], n),
-                    op=ALU.add,
-                )
+        by_head = "p (h d) -> p h d"
+
+        def add_planes(i, s, products):
+            nc.gpsimd.tensor_tensor(
+                out=result_of(i, s),
+                in0=products[:, 0, :].rearrange(by_head, d=HEAD_DIM),
+                in1=products[:, 1, :].rearrange(by_head, d=HEAD_DIM),
+                op=ALU.add,
+            )
 
         def copy_plain(copy, i, s, acc):
+            copy(out=result_of(i, s), in_=acc[:].rearrange(by_head, d=HEAD_DIM))
+
+        def finish(i, s):
             which, c = groups[i]
-            for column, n, head, feature in pieces(c):
-                copy(out=result_piece(which, s, n, head, feature), in_=by_head(acc[:, column : column + n], n))
+            pair = s // RUN
+            if s % RUN == RUN - 1:
+                for b in range(PAIR_BATCHES):
+                    heads = outputs[which][PAIR_BATCHES * pair + b, GROUP_HEADS * c : GROUP_HEADS * (c + 1)]
+                    nc.sync.dma_start(
+                        out=heads.rearrange("h (m r) d -> m h (r d)", r=RUN),
+                        in_=result_tiles[(i, pair)][b::PAIR_BATCHES].rearrange("p h r d -> p h (r d)"),
+                    )
 
-        def store(which, c, pair):
-            h0, h1 = heads_of(c)
-            result = result_of(which, pair, h0)[0]
-            for b in range(PAIR_BATCHES):
-                nc.sync.dma_start(
-                    out=outputs[which][PAIR_BATCHES * pair + b, h0:h1].rearrange("h (m r) d -> m h (r d)", r=RUN),
-                    in_=result[b::PAIR_BATCHES, 0 : h1 - h0].rearrange("p h r d -> p h (r d)"),
-                )
-
-        rot = const.tile([P, 2, SLOTS, TABLE_HEADS * HEAD_DIM], F32)
+        rot = const.tile([P, 2, SLOTS, GROUP_HEADS * HEAD_DIM], F32)
 
         def fill_table():
             nc.scalar.activation(
@@ -347,15 +316,10 @@ def tile_ropeattention_pa_kernel(tc, x, coords, W_qkv, out_0, out_1, out_2):
         def repeat_table(s):
             nc.vector.tensor_copy(
                 out=rot[:, :, s, HEAD_DIM:].rearrange("p i (h d) -> p i h d", d=HEAD_DIM),
-                in_=rot[:, :, s, :HEAD_DIM].unsqueeze(2).to_broadcast([P, 2, TABLE_HEADS - 1, HEAD_DIM]),
+                in_=rot[:, :, s, :HEAD_DIM].unsqueeze(2).to_broadcast([P, 2, GROUP_HEADS - 1, HEAD_DIM]),
             )
 
         by_scalar, by_vector = nc.scalar.copy, nc.vector.tensor_copy
-        by_pass = [(g, half) for g in range(PASSES) for half in range(2)]
-
-        def finish(i, s):
-            if s % RUN == RUN - 1:
-                store(*groups[i], s // RUN)
 
         rotated = [(i, s) for i in range(last + 1) if groups[i][0] != 2 for s in range(SLOTS)]
         plain = [(i, s) for i in range(last + 1) if groups[i][0] == 2 for s in range(SLOTS)]
@@ -363,17 +327,18 @@ def tile_ropeattention_pa_kernel(tc, x, coords, W_qkv, out_0, out_1, out_2):
         while rotated or plain:
             n = len(steps)
             units = []
-            for kind in ((rotated, rotated) if n % 3 == 1 or n < 2 else (plain, rotated)) if rotated else (plain, plain):
-                if kind and 2 * kind[0][0] <= n:
-                    units.append(kind.pop(0))
+            while rotated and rotated[0][0] <= n and len(units) < (4 if n == 0 else 3):
+                units.append(rotated.pop(0))
+            few = len(units)
+            while plain and plain[0][0] <= n and len(units) < (few + 1 if few > 1 else 4 if not rotated else 2):
+                units.append(plain.pop(0))
             steps.append(units)
 
         reduced = rotation_arguments(nc, const, coords_sb, freqs)
         flip_x(0, (by_scalar, by_scalar))
         quantise_x(0, (2, 1))
-        for half in range(2):
-            prepare(0, [(g, half) for g in range(PASSES)], ((by_scalar, by_scalar, by_vector), (by_scalar, by_scalar, by_vector))[half])
-            quantise_half(0, half)
+        prepare(0, WIDE + NARROW, (by_scalar, by_scalar, by_vector, by_scalar, by_scalar))
+        quantise(0, (1024, 128))
         flip_x(1, (by_scalar, by_scalar))
         angle = rotation_angles(nc, const, reduced)
         quantise_x(3, (2, 1))
@@ -384,44 +349,26 @@ def tile_ropeattention_pa_kernel(tc, x, coords, W_qkv, out_0, out_1, out_2):
         repeat_table(0)
         repeat_table(1)
 
-        late = []
         for n, units in enumerate(steps):
-            j, part = n // 2 + 1, n % 2
-            if j == 1:
-                prepare(j, [(g, part) for g in range(PASSES)], (by_scalar, by_scalar, by_scalar))
-            elif j <= last:
-                prepare(j, by_pass[3 * part : 3 * part + 3], (by_scalar, by_scalar, by_scalar))
+            if n + 1 <= last:
+                prepare(n + 1, WIDE + NARROW, (by_scalar,) * 5)
+                if n + 6 <= last:
+                    load_group(n + 6, whole)
             accs = [multiply(i, s) for i, s in units]
-            if j <= last:
-                if j == 1:
-                    quantise_half(j, part)
-                else:
-                    quantise(j, *((0, 1), (1, 3))[part])
-                if part == 1:
-                    for k in range(2):
-                        if to_load:
-                            load_half(*to_load.pop(0), 2)
-                if n >= 1 and n % 2 == 0:
-                    jj = (n + 3) // 2 + 1
-                    if jj <= last:
-                        spread_tile(by_scalar, jj, 1)
             if n == 0:
                 for s in (2, 3):
                     repeat_table(s)
-            for i, s, acc, products in late:
-                times_sin(i, s, acc, products)
-                add_planes(i, s, products)
-                finish(i, s)
-            late = []
-            for k, (i, s) in enumerate(units):
+            if n + 2 <= last:
+                spread_tile(by_scalar, n + 2, 2)
+                if n >= 1:
+                    spread_tile(by_vector, n + 2, 1)
+            for k, ((i, s), acc) in enumerate(zip(units, accs)):
+                if n + 1 <= last and k == min(1, len(units) - 1):
+                    quantise(n + 1, (1024, 128))
                 if groups[i][0] == 2:
-                    copy_plain(by_vector if n > 15 and k % 2 else by_scalar, i, s, accs[k])
-                    finish(i, s)
+                    copy_plain(by_scalar, i, s, acc)
                 else:
-                    products = times_cos(i, s, accs[k])
-                    if False:
-                        late.append((i, s, accs[k], products))
-                    else:
-                        times_sin(i, s, accs[k], products)
-                        add_planes(i, s, products, nc.vector if False else nc.gpsimd)
-                        finish(i, s)
+                    products = times_cos(i, s, acc)
+                    times_sin(i, s, acc, products)
+                    add_planes(i, s, products)
+                finish(i, s)

import math
from contextlib import ExitStack

import concourse.mybir as mybir
from concourse.masks import make_identity

F32 = mybir.dt.float32
BF16 = mybir.dt.bfloat16
U32 = mybir.dt.uint32
U8 = mybir.dt.uint8
FP8X4 = mybir.dt.float8_e4m3fn_x4
ALU = mybir.AluOpType
ACT = mybir.ActivationFunctionType

P = 128
BATCH = 4
TOKENS = 128
RUN = 2
PAIR_BATCHES = 2
SLOTS = 4
FEATURES = 1536
HEADS = 16
HEAD_DIM = 96
PAIRS = HEAD_DIM // 2
FREQS = HEAD_DIM // 6
K_PASS = 512
PASSES = FEATURES // K_PASS
PASS_WORDS = K_PASS // 2
OUT_COLS = HEADS * HEAD_DIM

GROUP_HEADS = 4
GROUP_COLS = GROUP_HEADS * HEAD_DIM
TILES = GROUP_COLS // P
QUARTERS = HEADS // GROUP_HEADS
PARTS = ((0, 2 * P), (2 * P, GROUP_COLS))

FLOPS = 2 * BATCH * P * FEATURES * 3 * OUT_COLS

TURN_HI = 6.28125
TURN_MID = 4059.0 / 2097152.0
TURN_LO = 2.0 * math.pi - TURN_HI - TURN_MID
ROUND_MAGIC = 12582912.0
PI_BELOW = 3.1415925


def frequencies(nc, const):
    freqs = const.tile([P, FREQS], F32)
    nc.vector.memset(freqs[:, 0:1], 1.0)
    n = 1
    while n < FREQS:
        nc.vector.tensor_scalar(
            out=freqs[:, n : 2 * n], in0=freqs[:, 0:n], scalar1=10000.0 ** (-n / FREQS), scalar2=None, op0=ALU.mult
        )
        n *= 2
    return freqs


def rotation_arguments(nc, const, coords_sb, freqs):
    theta = const.tile([P, SLOTS, PAIRS], F32)
    axes = [P, RUN * 3, FREQS]
    for pair in range(SLOTS // RUN):
        nc.vector.tensor_tensor(
            out=theta[:, RUN * pair : RUN * pair + RUN, :].rearrange("p r (a j) -> p (r a) j", j=FREQS),
            in0=coords_sb[:, pair, : RUN * 3].unsqueeze(2).to_broadcast(axes),
            in1=freqs[:].unsqueeze(1).to_broadcast(axes),
            op=ALU.mult,
        )

    turns = const.tile([P, SLOTS, PAIRS], F32)
    nc.vector.tensor_scalar(
        out=turns[:], in0=theta[:], scalar1=0.5 / math.pi, scalar2=ROUND_MAGIC, op0=ALU.mult, op1=ALU.add
    )
    nc.vector.tensor_scalar(out=turns[:], in0=turns[:], scalar1=ROUND_MAGIC, scalar2=None, op0=ALU.subtract)
    reduced = const.tile([P, SLOTS, PAIRS], F32)
    nc.vector.scalar_tensor_tensor(
        out=reduced[:], in0=turns[:], scalar=-TURN_HI, in1=theta[:], op0=ALU.mult, op1=ALU.add
    )
    for piece in (TURN_MID, TURN_LO):
        nc.vector.scalar_tensor_tensor(
            out=reduced[:], in0=turns[:], scalar=-piece, in1=reduced[:], op0=ALU.mult, op1=ALU.add
        )
    nc.vector.tensor_scalar(
        out=reduced[:], in0=reduced[:], scalar1=-PI_BELOW, scalar2=PI_BELOW, op0=ALU.max, op1=ALU.min
    )
    return reduced


def rotation_angles(nc, const, reduced):
    magnitude = const.tile([P, SLOTS, PAIRS], F32)
    nc.vector.scalar_tensor_tensor(
        out=magnitude[:], in0=reduced[:], scalar=-1.0, in1=reduced[:], op0=ALU.mult, op1=ALU.max
    )

    angle = const.tile([P, 2, SLOTS, PAIRS, 2], F32)
    nc.vector.tensor_scalar(
        out=angle[:, 0],
        in0=magnitude[:].unsqueeze(3).to_broadcast([P, SLOTS, PAIRS, 2]),
        scalar1=-1.0, scalar2=0.5 * math.pi, op0=ALU.mult, op1=ALU.add,
    )
    nc.vector.tensor_copy(out=angle[:, 1, :, :, 1], in_=reduced[:])
    nc.vector.tensor_scalar(out=angle[:, 1, :, :, 0], in0=reduced[:], scalar1=-1.0, scalar2=None, op0=ALU.mult)
    return angle


def tile_ropeattention_pa_kernel(tc, x, coords, W_qkv, out_0, out_1, out_2):
    nc = tc.nc
    outputs = (out_0, out_1, out_2)
    groups = [(which, c) for c in range(QUARTERS) for which in ((0, 2, 1) if c < QUARTERS - 1 else (0, 1, 2))]
    last = len(groups) - 1

    with ExitStack() as ctx:
        const = ctx.enter_context(tc.tile_pool(name="const", bufs=1))
        rows_pool = ctx.enter_context(tc.tile_pool(name="rows_pool", bufs=5))
        spread_pool = ctx.enter_context(tc.tile_pool(name="spread_pool", bufs=3))
        stage = ctx.enter_context(tc.tile_pool(name="stage", bufs=2))
        packed = ctx.enter_context(tc.tile_pool(name="packed", bufs=4))
        work = ctx.enter_context(tc.tile_pool(name="work", bufs=6))
        results = ctx.enter_context(tc.tile_pool(name="results", bufs=12))
        flip_psum = ctx.enter_context(tc.psum_pool(name="flip_psum", bufs=4))
        acc_psum = ctx.enter_context(tc.psum_pool(name="acc_psum", bufs=4))
        ctx.enter_context(tc.manual_schedule())

        def slot_rows(array, pair, b):
            return array[PAIR_BATCHES * pair + b].rearrange("(m r) k -> m r k", r=RUN)

        x_tiles = {}

        def load_x(pair, r0, r1):
            rows = const.tile([P, r1 - r0, FEATURES], BF16, name="x_%d_%d" % (pair, r0))
            for b in range(PAIR_BATCHES):
                nc.sync.dma_start(out=rows[b::PAIR_BATCHES], in_=slot_rows(x, pair, b)[:, r0:r1, :])
            for r in range(r0, r1):
                x_tiles[RUN * pair + r] = rows[:].bitcast(F32)[:, r - r0, :]

        w_rows = {}

        def load_group(i, cuts):
            which, c = groups[i]
            rows = rows_pool.tile([P, TILES, FEATURES], BF16, tag="rows")
            w_rows[i] = rows
            first = which * OUT_COLS + c * GROUP_COLS
            for t0, t1 in cuts:
                nc.sync.dma_start(
                    out=rows[:, t0:t1, :],
                    in_=W_qkv[first + t0 * P : first + t1 * P, :].rearrange("(t p) k -> p t k", p=P),
                )

        coords_sb = const.tile([P, SLOTS // RUN, 16], BF16)
        for pair in range(SLOTS // RUN):
            for b in range(PAIR_BATCHES):
                nc.scalar.dma_start(
                    out=coords_sb[b::PAIR_BATCHES, pair, : RUN * 3], in_=slot_rows(coords, pair, b).rearrange("m r a -> m (r a)")
                )
        load_x(0, 0, 1)
        load_group(0, [(t, t + 1) for t in range(TILES)])
        load_x(0, 1, 2)
        load_x(1, 0, 2)
        whole = [(0, TILES)]
        for i in range(1, 6):
            load_group(i, whole)

        freqs = frequencies(nc, const)
        warm = const.tile([P, 1], F32)
        nc.vector.memset(warm[:], 0.0)
        nc.scalar.activation(out=warm[:], in_=warm[:], func=ACT.Sin)

        identity = const.tile([P, P], F32)
        make_identity(nc, identity[:])

        x_codes = const.tile([P, SLOTS, PASSES, P], U32, align_bytes=64)
        x_scales = const.tile([P, SLOTS, PASSES, P], U8, align_bytes=64)
        x_grouped = const.tile([P, SLOTS, PASSES, 4 * P], BF16, align_bytes=64)

        def every_second(words, g, u):
            return words[:, PASS_WORDS * g + u : PASS_WORDS * (g + 1) : 2]

        def flip_x(s, copies):
            for (g0, g1), copy in zip(((0, 2), (2, 3)), copies):
                flipped = flip_psum.tile([P, g1 - g0, 2, P], F32, tag="flipped")
                for g in range(g0, g1):
                    for u in range(2):
                        nc.tensor.transpose(flipped[:, g - g0, u, :], every_second(x_tiles[s], g, u), identity[:])
                copy(
                    out=x_grouped[:, s, g0:g1, :].bitcast(F32).rearrange("q g (c u) -> q g c u", u=2),
                    in_=flipped[:].rearrange("q g u c -> q g c u"),
                )

        def quantise_x(first, widths):
            codes = x_codes[:].rearrange("q s g c -> q (s g c)")
            scales = x_scales[:].rearrange("q s g c -> q (s g c)")
            grouped = x_grouped[:].rearrange("q s g w -> q (s g w)")
            for n in widths:
                lo, hi = P * first, P * (first + n)
                nc.vector.quantize_mx(
                    out=codes[:, lo:hi].bitcast(FP8X4), scales=scales[:, lo:hi], in_=grouped[:, 4 * lo : 4 * hi]
                )
                first += n

        spread = {}

        def spread_tile(copy, i, t):
            tile = spread_pool.tile([P, 2, PASSES, P], F32, tag="spread")
            words = w_rows[i][:].bitcast(F32)[:, t, :]
            copy(out=tile[:], in_=words.rearrange("r (g q u) -> r u g q", g=PASSES, u=2))
            spread[(i, t)] = tile

        def tile_words(i, t, g, u):
            if (i, t) in spread:
                return spread[(i, t)][:, u, g, :]
            return every_second(w_rows[i][:].bitcast(F32)[:, t, :], g, u)

        operands = {}

        WIDE = [(g, g + 1, 0, 2) for g in range(PASSES)]
        NARROW = [(0, 2, 2, 3), (2, 3, 2, 3)]

        def prepare(i, banks, copies):
            if i not in operands:
                w_codes = packed.tile([P, PASSES, GROUP_COLS], U32, tag="w_codes", align_bytes=64)
                w_scales = packed.tile([P, PASSES, GROUP_COLS], U8, tag="w_scales", align_bytes=64)
                grouped = stage.tile([P, PASSES, 4 * GROUP_COLS], BF16, tag="grouped", align_bytes=64)
                operands[i] = (w_codes, w_scales, grouped)
            grouped = operands[i][2]
            for (g0, g1, t0, t1), copy in zip(banks, copies):
                flipped = flip_psum.tile([P, g1 - g0, 2, P * (t1 - t0)], F32, tag="flipped")
                for t in range(t0, t1):
                    for g in range(g0, g1):
                        for u in range(2):
                            nc.tensor.transpose(
                                flipped[:, g - g0, u, P * (t - t0) : P * (t - t0 + 1)], tile_words(i, t, g, u), identity[:]
                            )
                words = grouped[:, g0:g1, :].bitcast(F32)[:, :, 2 * P * t0 : 2 * P * t1]
                copy(out=words.rearrange("q g (c u) -> q g c u", u=2), in_=flipped[:].rearrange("q g u c -> q g c u"))

        def quantise(i, widths):
            w_codes, w_scales, grouped = operands[i]
            codes = w_codes[:].rearrange("q g c -> q (g c)")
            scales = w_scales[:].rearrange("q g c -> q (g c)")
            values = grouped[:].rearrange("q g w -> q (g w)")
            lo = 0
            for n in widths:
                nc.vector.quantize_mx(
                    out=codes[:, lo : lo + n].bitcast(FP8X4), scales=scales[:, lo : lo + n], in_=values[:, 4 * lo : 4 * (lo + n)]
                )
                lo += n

        def multiply(i, s):
            w_codes, w_scales, grouped = operands[i]
            acc = acc_psum.tile([P, GROUP_COLS], F32, tag="acc")
            for lo, hi in PARTS:
                for g in range(PASSES):
                    nc.tensor.matmul_mx(
                        out=acc[:, lo:hi],
                        lhsT=x_codes[:, s, g, :].bitcast(FP8X4),
                        lhsT_scale=x_scales[:, s, g, :],
                        rhs=w_codes[:, g, lo:hi].bitcast(FP8X4),
                        rhs_scale=w_scales[:, g, lo:hi],
                        start=(g == 0),
                        stop=(g == PASSES - 1),
                    )
            return acc

        result_tiles = {}

        def result_of(i, s):
            if (i, s // RUN) not in result_tiles:
                result = results.tile([P, GROUP_HEADS, RUN, HEAD_DIM], F32, tag="result")
                result_tiles[(i, s // RUN)] = result
            return result_tiles[(i, s // RUN)][:, :, s % RUN, :]

        def times_cos(i, s, acc):
            products = work.tile([P, 2, GROUP_COLS], F32, tag="products")
            nc.vector.tensor_tensor(out=products[:, 0, :], in0=acc[:], in1=rot[:, 0, s, :], op=ALU.mult)
            return products

        def times_sin(i, s, acc, products):
            in_pairs = "p (n w) -> p n w"
            nc.vector.tensor_tensor(
                out=products[:, 1, :].rearrange(in_pairs, w=2),
                in0=acc[:].rearrange(in_pairs, w=2)[:, :, ::-1],
                in1=rot[:, 1, s, :].rearrange(in_pairs, w=2),
                op=ALU.mult,
            )

        by_head = "p (h d) -> p h d"

        def add_planes(i, s, products):
            nc.gpsimd.tensor_tensor(
                out=result_of(i, s),
                in0=products[:, 0, :].rearrange(by_head, d=HEAD_DIM),
                in1=products[:, 1, :].rearrange(by_head, d=HEAD_DIM),
                op=ALU.add,
            )

        def copy_plain(copy, i, s, acc):
            copy(out=result_of(i, s), in_=acc[:].rearrange(by_head, d=HEAD_DIM))

        def finish(i, s):
            which, c = groups[i]
            pair = s // RUN
            if s % RUN == RUN - 1:
                for b in range(PAIR_BATCHES):
                    heads = outputs[which][PAIR_BATCHES * pair + b, GROUP_HEADS * c : GROUP_HEADS * (c + 1)]
                    nc.sync.dma_start(
                        out=heads.rearrange("h (m r) d -> m h (r d)", r=RUN),
                        in_=result_tiles[(i, pair)][b::PAIR_BATCHES].rearrange("p h r d -> p h (r d)"),
                    )

        rot = const.tile([P, 2, SLOTS, GROUP_HEADS * HEAD_DIM], F32)

        def fill_table():
            nc.scalar.activation(
                out=rot[:, :, :, :HEAD_DIM], in_=angle[:].rearrange("p i s n e -> p i s (n e)"), func=ACT.Sin
            )

        def repeat_table(s):
            nc.vector.tensor_copy(
                out=rot[:, :, s, HEAD_DIM:].rearrange("p i (h d) -> p i h d", d=HEAD_DIM),
                in_=rot[:, :, s, :HEAD_DIM].unsqueeze(2).to_broadcast([P, 2, GROUP_HEADS - 1, HEAD_DIM]),
            )

        by_scalar, by_vector = nc.scalar.copy, nc.vector.tensor_copy

        rotated = [(i, s) for i in range(last + 1) if groups[i][0] != 2 for s in range(SLOTS)]
        plain = [(i, s) for i in range(last + 1) if groups[i][0] == 2 for s in range(SLOTS)]
        steps = []
        while rotated or plain:
            n = len(steps)
            units = []
            while rotated and rotated[0][0] <= n and len(units) < (4 if n == 0 else 3):
                units.append(rotated.pop(0))
            few = len(units)
            while plain and plain[0][0] <= n and len(units) < (few + 1 if few > 1 else 4 if not rotated else 2):
                units.append(plain.pop(0))
            steps.append(units)

        reduced = rotation_arguments(nc, const, coords_sb, freqs)
        flip_x(0, (by_scalar, by_scalar))
        quantise_x(0, (2, 1))
        prepare(0, WIDE + NARROW, (by_scalar, by_scalar, by_vector, by_scalar, by_scalar))
        quantise(0, (1024, 128))
        flip_x(1, (by_scalar, by_scalar))
        angle = rotation_angles(nc, const, reduced)
        quantise_x(3, (2, 1))
        for s in (2, 3):
            flip_x(s, (by_scalar, by_scalar))
        quantise_x(6, (4, 2))
        fill_table()
        repeat_table(0)
        repeat_table(1)

        for n, units in enumerate(steps):
            if n + 1 <= last:
                prepare(n + 1, WIDE + NARROW, (by_scalar,) * 5)
                if n + 6 <= last:
                    load_group(n + 6, whole)
            accs = [multiply(i, s) for i, s in units]
            if n == 0:
                for s in (2, 3):
                    repeat_table(s)
            if n + 2 <= last:
                spread_tile(by_scalar, n + 2, 2)
                if n >= 1:
                    spread_tile(by_vector, n + 2, 1)
            for k, ((i, s), acc) in enumerate(zip(units, accs)):
                if n + 1 <= last and k == min(1, len(units) - 1):
                    quantise(n + 1, (1024, 128))
                if groups[i][0] == 2:
                    copy_plain(by_scalar, i, s, acc)
                else:
                    products = times_cos(i, s, acc)
                    times_sin(i, s, acc, products)
                    add_planes(i, s, products)
                finish(i, s)
